import numpy as np
import ml_dtypes


def mxq(x, axis, fmt="e4m3"):
    dtype, down = {"e4m3": (ml_dtypes.float8_e4m3fn, 7), "e5m2": (ml_dtypes.float8_e5m2, 14)}[fmt]
    v = np.moveaxis(np.asarray(x, np.float32).astype(ml_dtypes.bfloat16).astype(np.float64), axis, -1)
    blocks = v.reshape(v.shape[:-1] + (-1, 32))
    amax = np.abs(blocks).max(-1, keepdims=True)
    byte = np.maximum(np.where(amax > 0, np.frexp(amax)[1] - 1 + 127, 0) - down, 1)
    scale = np.exp2(byte - 127.0)
    codes = (blocks / scale).astype(np.float32).astype(dtype).astype(np.float64)
    return np.moveaxis((codes * scale).reshape(v.shape), -1, axis)


WIDE = False


def mx_kscale(k):
    if not WIDE:
        return np.ones(k)
    levels = np.array([10, -10, 5, -5, 0])
    if k % 512:
        return np.exp2(np.random.permutation(np.resize(levels, k // 32))).repeat(32)
    a = np.empty((k // 512, 16))
    for p in range(k // 512):
        a[p, :8] = np.random.permutation(np.resize(levels, 8))
        for g in range(8):
            far = levels[np.abs(levels - a[p, g]) >= 10]
            a[p, g + 8] = far[np.random.randint(len(far))]
    return np.exp2(a.ravel()).repeat(32)


BF16 = ml_dtypes.bfloat16


def bf(x):
    return np.asarray(x, np.float32).astype(BF16)


def f64(x):
    return np.asarray(x).astype(np.float64)


E2M1 = np.array([0.0, 0.5, 1.0, 1.5, 2.0, 3.0, 4.0, 6.0, -0.0, -0.5, -1.0, -1.5, -2.0, -3.0, -4.0, -6.0])


def pack_weight(w, fmt):
    k, n = w.shape
    w = f64(bf(w)).reshape(k // 32, 32, n)
    amax = np.abs(w).max(1)
    if fmt == "e4m3":
        byte = np.frexp(amax)[1] - 1 + 127 - 7
    else:
        mant, ex = np.frexp(amax / 6.0)
        byte = np.where(mant > 0.5, ex, ex - 1) + 127
    byte = np.clip(np.where(amax > 0, byte, 1), 1, 254)
    scaled = (w * np.exp2(127.0 - byte)[:, None, :]).reshape(k, n).astype(np.float32)
    by_word = np.ascontiguousarray(scaled.reshape(k // 512, 128, 4, n).transpose(0, 1, 3, 2))
    if fmt == "e4m3":
        words = by_word.astype(ml_dtypes.float8_e4m3fn).view(np.uint8)
    else:
        c = by_word.astype(ml_dtypes.float4_e2m1fn).view(np.uint8) & 0xF
        words = c[..., 0::2] | (c[..., 1::2] << 4)
    return np.ascontiguousarray(words), np.ascontiguousarray(byte.astype(np.uint8).reshape(k // 512, 16, n))


def unpack_weight(words, scales, fmt):
    g, p, n, _ = words.shape
    if fmt == "e4m3":
        vals = np.ascontiguousarray(words).view(ml_dtypes.float8_e4m3fn).astype(np.float64)
    else:
        nib = np.empty((g, p, n, 4), np.uint8)
        nib[..., 0::2] = words & 0xF
        nib[..., 1::2] = words >> 4
        vals = E2M1[nib]
    vals = vals * np.repeat(np.exp2(scales.astype(np.float64) - 127.0), 8, axis=1)[..., None]
    return vals.transpose(0, 1, 3, 2).reshape(g * 512, n)
def pack4(w):
    words, scales = pack_weight(w, "e2m1")
    return words.reshape(words.shape[0], 128, -1), scales


def unpack4(words, scales):
    return unpack_weight(words.reshape(words.shape[0], 128, -1, 2), scales, "e2m1")


B, T, D, H, KH, F = 2, 128, 1024, 8, 2, 4096
EPS = 1e-5


def layer_norm(v, g, b):
    m = v.mean(-1, keepdims=True)
    var = ((v - m) ** 2).mean(-1, keepdims=True)
    return (v - m) / np.sqrt(var + EPS) * g + b


def draw0():
    s, t = mx_kscale(D), mx_kscale(D)
    h_attn = bf(np.random.standard_normal((B, T, D)) * 0.4 * s)
    x = bf(np.random.standard_normal((B, T, D)))
    Wo_words, Wo_scales = pack4(np.random.standard_normal((D, D)) * 2.0 / np.sqrt(D) / s[:, None])
    bo = bf(np.random.standard_normal(D) * 0.2)
    ln2_g = bf(1.5 + 0.3 * np.random.standard_normal(D))
    ln2_b = bf(0.3 + 0.3 * np.random.standard_normal(D))
    fln_g = bf((1.0 + 0.1 * np.random.standard_normal(D)) * t)
    fln_b = bf(0.2 * np.random.standard_normal(D) * t)
    W1_words, W1_scales = pack4(np.random.standard_normal((D, F)) / np.sqrt(D) / t[:, None])
    b1 = bf(np.random.standard_normal(F) * 0.3)
    W2_words, W2_scales = pack4(np.random.standard_normal((D, F)) / np.sqrt(D) / t[:, None])
    b2 = bf(np.random.standard_normal(F) * 0.3)
    return {
        "h_attn": h_attn,
        "x": x,
        "Wo_words": Wo_words,
        "Wo_scales": Wo_scales,
        "bo": bo,
        "ln2_g": ln2_g,
        "ln2_b": ln2_b,
        "fln_g": fln_g,
        "fln_b": fln_b,
        "W1_words": W1_words,
        "W1_scales": W1_scales,
        "b1": b1,
        "W2_words": W2_words,
        "W2_scales": W2_scales,
        "b2": b2,
    }


def core(h_attn, x, Wo_words, Wo_scales, bo, ln2_g, ln2_b, fln_g, fln_b, W1_words, W1_scales, b1, W2_words, W2_scales, b2):
    y = f64(x) + ((mxq(f64(h_attn), 2, "e4m3") @ unpack4(Wo_words, Wo_scales)) + f64(bo))
    r = layer_norm(y, f64(ln2_g), f64(ln2_b))
    h2q = mxq(layer_norm(r, f64(fln_g), f64(fln_b)), 2, "e4m3")
    g_pre = (h2q @ unpack4(W1_words, W1_scales)) + f64(b1)
    hidden = (h2q @ unpack4(W2_words, W2_scales)) + f64(b2)
    return r, g_pre, hidden


def e4m3fn_bytes(y):
    return np.clip(np.asarray(y, np.float64), -448.0, 448.0).astype(np.float32).astype(ml_dtypes.float8_e4m3fn).view(np.uint8)


def e4m3fn_values(b):
    return np.asarray(b, np.uint8).view(ml_dtypes.float8_e4m3fn).astype(np.float64)


def setup_inputs():
    d = draw0()
    x0 = np.asarray(d['h_attn']).astype(np.float64)
    s = (np.max(np.abs(x0), axis=(0, 1), keepdims=True) / 448.0).astype(np.float32)
    out = {}
    for k, v in d.items():
        if k == 'h_attn':
            out['h_attn_bytes'] = e4m3fn_bytes(x0 / s.astype(np.float64))
            out['h_attn_scale'] = s
        else:
            out[k] = v
    return out


def reference(h_attn_bytes, h_attn_scale, x, Wo_words, Wo_scales, bo, ln2_g, ln2_b, fln_g, fln_b, W1_words, W1_scales, b1, W2_words, W2_scales, b2):
    return core(e4m3fn_values(h_attn_bytes) * h_attn_scale.astype(np.float64), x, Wo_words, Wo_scales, bo, ln2_g, ln2_b, fln_g, fln_b, W1_words, W1_scales, b1, W2_words, W2_scales, b2)

@@ -1,0 +1,383 @@
+from contextlib import ExitStack
+
+import concourse.mybir as mybir
+from concourse.masks import make_identity
+
+F32 = mybir.dt.float32
+BF16 = mybir.dt.bfloat16
+I32 = mybir.dt.int32
+U32 = mybir.dt.uint32
+U8 = mybir.dt.uint8
+FP8 = mybir.dt.float8_e4m3fn
+FP8X4 = mybir.dt.float8_e4m3fn_x4
+FP4X4 = mybir.dt.float4_e2m1fn_x4
+ADD = mybir.AluOpType.add
+MULT = mybir.AluOpType.mult
+ACT = mybir.ActivationFunctionType
+
+B, T, D, F = 2, 128, 1024, 4096
+P = 128
+G = 2
+HALF = 512
+EPS = 1e-5
+
+FLOPS = 2 * B * T * D * (D + 2 * F)
+
+
+def tile_transformerblock_pa_w4_kernel(
+    tc, h_bytes, h_scale, x, wo_words, wo_scales, bo, ln2_g, ln2_b, fln_g, fln_b,
+    w1_words, w1_scales, b1, w2_words, w2_scales, b2, out_r, out_1, out_2,
+):
+    nc = tc.nc
+    with ExitStack() as ctx:
+        sb = ctx.enter_context(tc.tile_pool(name="sb", bufs=1))
+        ps = ctx.enter_context(tc.psum_pool(name="ps", bufs=1))
+        ctx.enter_context(tc.manual_schedule())
+
+        def bank(i, shape, dtype, name):
+            return ps.tile(shape, dtype, tag="bank%d" % i, name=name)
+
+        def st(name, w=1):
+            return sb.tile([P, w], F32, name=name)
+
+        vrows = sb.tile([P, D], BF16, name="vrows")
+        wos = sb.tile([P, G, D], U8, name="wos", align_bytes=64)
+        w1s = sb.tile([P, G, F], U8, name="w1s", align_bytes=64)
+        w2s = sb.tile([P, G, F], U8, name="w2s", align_bytes=64)
+        ident_f = sb.tile([P, P], F32, name="ident_f")
+        ident_b = sb.tile([P, P], BF16, name="ident_b")
+        zero = sb.tile([P, HALF], BF16, name="zero")
+        one = st("one")
+        junk1 = st("junk1")
+
+        nc.gpsimd.memset(vrows[:].bitcast(I32), 0)
+        nc.vector.memset(one[:], 1.0)
+        nc.vector.memset(zero[:].bitcast(I32), 0)
+        nc.vector.memset(wos[:].rearrange("p g n -> p (g n)").bitcast(I32), 0)
+        make_identity(nc, ident_f[:])
+        make_identity(nc, ident_b[:])
+        nc.vector.memset(w1s[:, 0, :].bitcast(I32), 0)
+        nc.gpsimd.memset(w1s[:, 1, :].bitcast(I32), 0)
+
+        hb = [sb.tile([P, D], U8, name="hb%d" % b, align_bytes=64) for b in range(B)]
+        hs = sb.tile([P, G, 4], F32, name="hs")
+        xt = [sb.tile([P, D], BF16, name="xt%d" % b) for b in range(B)]
+        wo = sb.tile([P, G, 2 * D], U8, name="wo", align_bytes=64)
+        wc = [[sb.tile([P, G, 2048], U8, name="w%d_%d" % (w, c), align_bytes=64) for c in range(4)] for w in range(2)]
+        b1_sb = sb.tile([P, F], BF16, name="b1_sb")
+        b2_sb = sb.tile([P, F], BF16, name="b2_sb")
+        bo_sb = sb.tile([P, D], BF16, name="bo_sb")
+
+        def load_scales(dst, src):
+            s32 = src.bitcast(I32).rearrange("g (q r) n -> r q g n", r=4)
+            for r in range(4):
+                nc.sync.dma_start(out=dst[r:P:32, :, :].bitcast(I32), in_=s32[r])
+
+        def load_chunk(w, c):
+            src = (w1_words, w2_words)[w][:, :, 2048 * c : 2048 * (c + 1)].bitcast(I32)
+            nc.sync.dma_start(out=wc[w][c][:].bitcast(I32), in_=src.rearrange("g p n -> p g n"))
+
+        nc.sync.dma_start(out=hb[0][:], in_=h_bytes[0])
+        nc.scalar.dma_start(out=hs[:], in_=h_scale.rearrange("a o (g p t) -> p (a o g) t", p=P, t=4))
+        nc.scalar.activation(out=junk1[:], in_=one[:], func=ACT.Abs_reciprocal_sqrt, bias=EPS, scale=1.0)
+        nc.sync.dma_start(out=hb[1][:], in_=h_bytes[1])
+        nc.sync.dma_start(out=xt[0][:], in_=x[0])
+        nc.sync.dma_start(out=bo_sb[:], in_=bo.partition_broadcast(P))
+        for row, vec in enumerate((bo, ln2_g, ln2_b, fln_g, fln_b)):
+            if row:
+                nc.scalar.dma_start(out=vrows[row : row + 1, :], in_=vec.rearrange("(o c) -> o c", o=1))
+        nc.scalar.dma_start(out=vrows[5:9, :], in_=b1.rearrange("(r c) -> r c", r=4))
+        for g in range(G):
+            nc.sync.dma_start(out=wo[:, g, :].bitcast(I32), in_=wo_words[g].bitcast(I32))
+        load_scales(wos, wo_scales)
+        nc.sync.dma_start(out=xt[1][:], in_=x[1])
+        load_scales(w1s, w1_scales)
+        for c in range(4):
+            load_chunk(0, c)
+        for c in range(4):
+            load_chunk(1, c)
+        nc.sync.dma_start(out=b2_sb[:], in_=b2.partition_broadcast(P))
+
+        hbf = [sb.tile([P, D], BF16, name="hbf%d" % b, align_bytes=64) for b in range(B)]
+        hT = [None, None]
+        qin = [sb.tile([P, G, P, 4], BF16, name="qin%d" % b, align_bytes=64) for b in range(B)]
+        codes = [sb.tile([P, G, P], U32, name="codes%d" % b, align_bytes=64) for b in range(B)]
+        scal = [sb.tile([P, G, P], U8, name="scal%d" % b, align_bytes=64) for b in range(B)]
+        qin2 = [sb.tile([P, G, P, 4], BF16, name="qin2_%d" % b, align_bytes=64) for b in range(B)]
+        codes2 = [sb.tile([P, G, P], U32, name="codes2_%d" % b, align_bytes=64) for b in range(B)]
+        scal2 = [sb.tile([P, G, P], U8, name="scal2_%d" % b, align_bytes=64) for b in range(B)]
+        xb = [sb.tile([P, D], F32, name="xb%d" % b) for b in range(B)]
+        y = [sb.tile([P, D], F32, name="y%d" % b) for b in range(B)]
+        u = [sb.tile([P, D], F32, name="u%d" % b) for b in range(B)]
+        r = [sb.tile([P, D], F32, name="r%d" % b) for b in range(B)]
+        v = [sb.tile([P, D], F32, name="v%d" % b) for b in range(B)]
+        h2 = [sb.tile([P, D], BF16, name="h2_%d" % b, align_bytes=64) for b in range(B)]
+        sq = sb.tile([P, D], BF16, name="sq")
+        acc = [[None, None], [None, None]]
+        sl = [slice(0, HALF), slice(HALF, D)]
+
+        def transposes(dst, src, gs):
+            words = src[:].bitcast(F32)
+            for g in gs:
+                for k in range(2):
+                    nc.tensor.transpose(dst[g][:, k, :], words[:, 256 * g + k : 256 * (g + 1) : 2], ident_f[:])
+
+        def bcast(dst, row):
+            for i in range(2):
+                nc.tensor.matmul(
+                    dst[:, sl[i]], lhsT=ident_b[:, row : row + 1].to_broadcast([P, P]), rhs=vrows[:, sl[i]],
+                    start=True, stop=True,
+                )
+
+        def scale_rows(b, g):
+            src = hT[b][g][:].bitcast(BF16).rearrange("p k (n e) -> p n k e", e=2)
+            fac = hs[:, g, :].rearrange("p (k e) -> p k e", e=2).unsqueeze(1).to_broadcast([P, P, 2, 2])
+            nc.vector.tensor_tensor(
+                out=qin[b][:, g, :, :].rearrange("p n (k e) -> p n k e", e=2), in0=src, in1=fac, op=MULT
+            )
+
+        def quant(dst, sc, src, g):
+            nc.vector.quantize_mx(
+                out=dst[:, g, :].bitcast(FP8X4), scales=sc[:, g, :], in_=src[:, g, :, :].rearrange("p n t -> p (n t)")
+            )
+
+        def mm1(b, k0, k1):
+            for n, kb in enumerate((k0, k1)):
+                acc[b][n] = bank(kb, [P, HALF], F32, "acc%d_%d" % (b, n))
+                for g in range(G):
+                    nc.tensor.matmul_mx(
+                        out=acc[b][n][:],
+                        lhsT=codes[b][:, g, :].bitcast(FP8X4), lhsT_scale=scal[b][:, g, :],
+                        rhs=wo[:, g, 1024 * n : 1024 * (n + 1)].bitcast(FP4X4), rhs_scale=wos[:, g, sl[n]],
+                        start=(g == 0), stop=(g == G - 1),
+                    )
+
+        ysum = [st("ysum%d" % b, 2) for b in range(B)]
+        rsum = [st("rsum%d" % b, 2) for b in range(B)]
+        nmy = [st("nmy%d" % b) for b in range(B)]
+        nmr = [st("nmr%d" % b) for b in range(B)]
+        ssy = [st("ssy%d" % b) for b in range(B)]
+        ssr = [st("ssr%d" % b) for b in range(B)]
+        rsy = [st("rsy%d" % b) for b in range(B)]
+        rsr = [st("rsr%d" % b) for b in range(B)]
+
+        def do_y(b, n):
+            nc.vector.scalar_tensor_tensor(
+                out=y[b][:, sl[n]], in0=acc[b][n][:], scalar=1.0, in1=xb[b][:, sl[n]], op0=MULT, op1=ADD,
+                accum_out=ysum[b][:, n : n + 1],
+            )
+
+        def negmean(dst, sums):
+            nc.vector.tensor_scalar(out=dst[:], in0=sums[:, 0:1], scalar1=sums[:, 1:2], scalar2=-1.0 / D, op0=ADD, op1=MULT)
+
+        def rstd(dst, ss, src, nm):
+            nc.scalar.activation(out=sq[:], in_=src[:], func=ACT.Square, bias=nm[:], scale=1.0, accum_out=ss[:])
+            nc.scalar.activation(out=dst[:], in_=ss[:], func=ACT.Abs_reciprocal_sqrt, bias=EPS, scale=1.0 / D)
+
+        def do_u(b, n):
+            nc.vector.scalar_tensor_tensor(
+                out=u[b][:, sl[n]], in0=y[b][:, sl[n]], scalar=nmy[b][:], in1=lng[:, sl[n]], op0=ADD, op1=MULT)
+
+        def do_r(b, n):
+            nc.vector.scalar_tensor_tensor(
+                out=r[b][:, sl[n]], in0=u[b][:, sl[n]], scalar=rsy[b][:], in1=lnb[:, sl[n]], op0=MULT, op1=ADD,
+                accum_out=rsum[b][:, n : n + 1])
+
+        def do_v(b, n):
+            nc.vector.scalar_tensor_tensor(
+                out=v[b][:, sl[n]], in0=r[b][:, sl[n]], scalar=nmr[b][:], in1=fg[:, sl[n]], op0=ADD, op1=MULT)
+
+        def do_h(b, n):
+            nc.vector.scalar_tensor_tensor(
+                out=h2[b][:, sl[n]], in0=v[b][:, sl[n]], scalar=rsr[b][:], in1=fb[:, sl[n]], op0=MULT, op1=ADD)
+
+        def evac_h(b, g):
+            nc.scalar.copy(
+                out=qin2[b][:, g, :, :].rearrange("p n t -> p (n t)").bitcast(F32).rearrange("p (n k) -> p n k", k=2),
+                in_=h2T[b][g][:].rearrange("p k n -> p n k"))
+
+        def bias_chunk(c, kb):
+            t = bank(kb, [P, D], BF16, "bias%d" % c)
+            bcast(t, 5 + c)
+            nc.scalar.copy(out=b1_sb[:, D * c : D * (c + 1)], in_=t[:])
+
+        o = {}
+        outs = (out_1, out_2)
+        blk_ps = {}
+
+        def mm2(j, banks):
+            b, w, c = j // 8, (j // 4) % 2, j % 4
+            ws = (w1s, w2s)[w]
+            tiles = [bank(banks[n], [P, HALF], F32, "blk%d_%d" % (j, n)) for n in range(2)]
+            blk_ps[j] = tiles
+            for g in range(G):
+                for n in range(2):
+                    nc.tensor.matmul_mx(
+                        out=tiles[n][:],
+                        lhsT=codes2[b][:, g, :].bitcast(FP8X4), lhsT_scale=scal2[b][:, g, :],
+                        rhs=wc[w][c][:, g, 1024 * n : 1024 * (n + 1)].bitcast(FP4X4),
+                        rhs_scale=ws[:, g, D * c + HALF * n : D * c + HALF * (n + 1)],
+                        start=(g == 0), stop=(g == G - 1),
+                    )
+            o[j] = sb.tile([P, D], F32, name="o%d" % j)
+
+        def bias_of(j, n):
+            w, c = (j // 4) % 2, j % 4
+            return (b1_sb, b2_sb)[w][:, D * c + HALF * n : D * c + HALF * (n + 1)]
+
+        def evac_v(j, n):
+            nc.vector.tensor_tensor(out=o[j][:, sl[n]], in0=blk_ps[j][n][:], in1=bias_of(j, n), op=ADD)
+
+        def evac_s(j):
+            for n in range(2):
+                nc.scalar.copy(out=o[j][:, sl[n]], in_=blk_ps[j][n][:])
+            for n in range(2):
+                nc.gpsimd.tensor_tensor(out=o[j][:, sl[n]], in0=o[j][:, sl[n]], in1=bias_of(j, n), op=ADD)
+
+        def store(j, n=None):
+            b, w, c = j // 8, (j // 4) % 2, j % 4
+            cols = slice(0, D) if n is None else sl[n]
+            nc.sync.dma_start(out=outs[w][b, :, D * c + cols.start : D * c + cols.stop], in_=o[j][:, cols])
+
+        def t_banks(ks, name):
+            return [bank(ks[g], [P, 2, P], F32, "%s_%d" % (name, g)) for g in range(G)]
+
+        def do_xb(eng, b, n):
+            eng.tensor_tensor(out=xb[b][:, sl[n]], in0=xt[b][:, sl[n]], in1=bo_sb[:, sl[n]], op=ADD)
+
+        warm = bank(3, [P, HALF], F32, "warm")
+        for i in range(6):
+            nc.tensor.matmul(warm[:], lhsT=zero[:, 0:P], rhs=zero[:], start=True, stop=True)
+        for b in range(B):
+            nc.vector.tensor_copy(out=hbf[b][:, sl[0]], in_=hb[b][:, sl[0]].bitcast(FP8))
+            nc.scalar.copy(out=hbf[b][:, sl[1]], in_=hb[b][:, sl[1]].bitcast(FP8))
+        for b in range(B):
+            for n in range(2):
+                do_xb(nc.gpsimd, b, n)
+        nc.gpsimd.memset(w2s[:].rearrange("p g n -> p (g n)").bitcast(I32), 0)
+        load_scales(w2s, w2_scales)
+        hT[0] = t_banks((0, 1), "hT0")
+        transposes(hT[0], hbf[0], (0, 1))
+        hT[1] = t_banks((5, 6), "hT1")
+        transposes(hT[1], hbf[1], (0, 1))
+        bias_chunk(0, 2)
+        bias_chunk(1, 7)
+        scale_rows(0, 0)
+        scale_rows(0, 1)
+        quant(codes[0], scal[0], qin[0], 0)
+        quant(codes[0], scal[0], qin[0], 1)
+        mm1(0, 3, 4)
+        scale_rows(1, 0)
+        scale_rows(1, 1)
+        lng = bank(0, [P, D], BF16, "lng")
+        bcast(lng, 1)
+        lnb = bank(1, [P, D], BF16, "lnb")
+        bcast(lnb, 2)
+
+        do_y(0, 0)
+        do_y(0, 1)
+        quant(codes[1], scal[1], qin[1], 0)
+        negmean(nmy[0], ysum[0])
+        quant(codes[1], scal[1], qin[1], 1)
+        rstd(rsy[0], ssy[0], y[0], nmy[0])
+        mm1(1, 5, 6)
+        bias_chunk(2, 3)
+        fg = bank(2, [P, D], BF16, "fg")
+        bcast(fg, 3)
+        do_u(0, 0)
+        do_u(0, 1)
+        do_y(1, 0)
+        do_r(0, 0)
+        do_r(0, 1)
+        bias_chunk(3, 4)
+        fb = bank(7, [P, D], BF16, "fb")
+        bcast(fb, 4)
+        negmean(nmr[0], rsum[0])
+        rstd(rsr[0], ssr[0], r[0], nmr[0])
+        nc.sync.dma_start(out=out_r[0], in_=r[0][:])
+        do_v(0, 0)
+        do_v(0, 1)
+        do_y(1, 1)
+        negmean(nmy[1], ysum[1])
+        rstd(rsy[1], ssy[1], y[1], nmy[1])
+        do_h(0, 0)
+        do_h(0, 1)
+        h2T = [None, None]
+        h2T[0] = t_banks((3, 4), "h2T0")
+        transposes(h2T[0], h2[0], (0,))
+        evac_h(0, 0)
+        transposes(h2T[0], h2[0], (1,))
+        evac_h(0, 1)
+        warm2 = bank(5, [P, HALF], F32, "warm2")
+        for i in range(2):
+            nc.tensor.matmul(warm2[:], lhsT=zero[:, 0:P], rhs=zero[:], start=True, stop=True)
+        do_u(1, 0)
+        quant(codes2[0], scal2[0], qin2[0], 0)
+        do_u(1, 1)
+        quant(codes2[0], scal2[0], qin2[0], 1)
+
+        mm2(0, (6, 5))
+        do_r(1, 0)
+        do_r(1, 1)
+        nc.sync.dma_start(out=out_r[1], in_=r[1][:])
+        evac_v(0, 0)
+        store(0, 0)
+        negmean(nmr[1], rsum[1])
+        evac_v(0, 1)
+        store(0, 1)
+        mm2(1, (3, 4))
+        evac_s(1)
+        rstd(rsr[1], ssr[1], r[1], nmr[1])
+        mm2(2, (6, 5))
+        do_v(1, 0)
+        evac_v(2, 0)
+        store(2, 0)
+        store(1, 0)
+        evac_v(2, 1)
+        store(2, 1)
+        store(1, 1)
+        mm2(3, (0, 1))
+        evac_s(3)
+        do_v(1, 1)
+        do_h(1, 0)
+        mm2(4, (3, 4))
+        evac_v(4, 0)
+        evac_v(4, 1)
+        store(4, 0)
+        store(3, 0)
+        store(4, 1)
+        store(3, 1)
+        do_h(1, 1)
+        mm2(5, (6, 5))
+        mm2(6, (0, 1))
+        h2T[1] = t_banks((2, 7), "h2T1")
+        transposes(h2T[1], h2[1], (0, 1))
+        evac_h(1, 0)
+        evac_h(1, 1)
+        evac_v(5, 0)
+        quant(codes2[1], scal2[1], qin2[1], 0)
+        evac_v(5, 1)
+        quant(codes2[1], scal2[1], qin2[1], 1)
+        store(5)
+        mm2(7, (3, 4))
+        evac_s(6)
+        evac_v(7, 0)
+        evac_v(7, 1)
+        store(7)
+        plan = {8: "v", 9: "s", 10: "v", 11: "v", 12: "s", 13: "v", 14: "v", 15: "v"}
+        cyc = [(6, 5), (2, 7), (0, 1), (3, 4)]
+        late = [6]
+        for i, j in enumerate(range(8, 16)):
+            mm2(j, cyc[i % 4])
+            if plan[j] == "s":
+                evac_s(j)
+                late.append(j)
+            else:
+                for n in range(2):
+                    evac_v(j, n)
+                    if j >= 14:
+                        store(j, n)
+                if j < 14:
+                    store(j)
+                if late and j != 10 and j != 13:
+                    store(late.pop(0))

@@ -51,21 +51,21 @@ def tile_transformerblock_pa_w4_kernel(
         junk1 = st("junk1")
 
         nc.gpsimd.memset(vrows[:].bitcast(I32), 0)
+        nc.vector.memset(wos[:].rearrange("p g n -> p (g n)").bitcast(I32), 0)
         nc.vector.memset(one[:], 1.0)
         nc.vector.memset(zero[:].bitcast(I32), 0)
-        nc.vector.memset(wos[:].rearrange("p g n -> p (g n)").bitcast(I32), 0)
         make_identity(nc, ident_f[:])
         make_identity(nc, ident_b[:])
         nc.vector.memset(w1s[:, 0, :].bitcast(I32), 0)
         nc.gpsimd.memset(w1s[:, 1, :].bitcast(I32), 0)
+        nc.gpsimd.memset(w2s[:].rearrange("p g n -> p (g n)").bitcast(I32), 0)
 
         hb = [sb.tile([P, D], U8, name="hb%d" % b, align_bytes=64) for b in range(B)]
         hs = sb.tile([P, G, 4], F32, name="hs")
         xt = [sb.tile([P, D], BF16, name="xt%d" % b) for b in range(B)]
         wo = sb.tile([P, G, 2 * D], U8, name="wo", align_bytes=64)
         wc = [[sb.tile([P, G, 2048], U8, name="w%d_%d" % (w, c), align_bytes=64) for c in range(4)] for w in range(2)]
-        b1_sb = sb.tile([P, F], BF16, name="b1_sb")
-        b2_sb = sb.tile([P, F], BF16, name="b2_sb")
+        b12 = sb.tile([P, 2 * F], BF16, name="b12")
         bo_sb = sb.tile([P, D], BF16, name="bo_sb")
 
         def load_scales(dst, src):
@@ -82,21 +82,21 @@ def tile_transformerblock_pa_w4_kernel(
         nc.scalar.activation(out=junk1[:], in_=one[:], func=ACT.Abs_reciprocal_sqrt, bias=EPS, scale=1.0)
         nc.sync.dma_start(out=hb[1][:], in_=h_bytes[1])
         nc.sync.dma_start(out=xt[0][:], in_=x[0])
-        nc.sync.dma_start(out=bo_sb[:], in_=bo.partition_broadcast(P))
         for row, vec in enumerate((bo, ln2_g, ln2_b, fln_g, fln_b)):
-            if row:
-                nc.scalar.dma_start(out=vrows[row : row + 1, :], in_=vec.rearrange("(o c) -> o c", o=1))
+            nc.scalar.dma_start(out=vrows[row : row + 1, :], in_=vec.rearrange("(o c) -> o c", o=1))
         nc.scalar.dma_start(out=vrows[5:9, :], in_=b1.rearrange("(r c) -> r c", r=4))
+        nc.scalar.dma_start(out=vrows[9:11, :], in_=b2[0 : 2 * D].rearrange("(r c) -> r c", r=2))
+        load_scales(wos, wo_scales)
         for g in range(G):
             nc.sync.dma_start(out=wo[:, g, :].bitcast(I32), in_=wo_words[g].bitcast(I32))
-        load_scales(wos, wo_scales)
         nc.sync.dma_start(out=xt[1][:], in_=x[1])
         load_scales(w1s, w1_scales)
         for c in range(4):
             load_chunk(0, c)
+        load_scales(w2s, w2_scales)
         for c in range(4):
             load_chunk(1, c)
-        nc.sync.dma_start(out=b2_sb[:], in_=b2.partition_broadcast(P))
+        nc.sync.dma_start(out=b12[:, 6 * D : 8 * D], in_=b2[2 * D : 4 * D].partition_broadcast(P))
 
         hbf = [sb.tile([P, D], BF16, name="hbf%d" % b, align_bytes=64) for b in range(B)]
         hT = [None, None]
@@ -128,6 +128,12 @@ def tile_transformerblock_pa_w4_kernel(
                     dst[:, sl[i]], lhsT=ident_b[:, row : row + 1].to_broadcast([P, P]), rhs=vrows[:, sl[i]],
                     start=True, stop=True,
                 )
+
+        def bcast_half(dst, row, n):
+            nc.tensor.matmul(
+                dst[:], lhsT=ident_b[:, row : row + 1].to_broadcast([P, P]), rhs=vrows[:, sl[n]],
+                start=True, stop=True,
+            )
 
         def scale_rows(b, g):
             src = hT[b][g][:].bitcast(BF16).rearrange("p k (n e) -> p n k e", e=2)
@@ -196,10 +202,16 @@ def tile_transformerblock_pa_w4_kernel(
                 out=qin2[b][:, g, :, :].rearrange("p n t -> p (n t)").bitcast(F32).rearrange("p (n k) -> p n k", k=2),
                 in_=h2T[b][g][:].rearrange("p k n -> p n k"))
 
-        def bias_chunk(c, kb):
+        def chunk_mm(c, kb):
             t = bank(kb, [P, D], BF16, "bias%d" % c)
             bcast(t, 5 + c)
-            nc.scalar.copy(out=b1_sb[:, D * c : D * (c + 1)], in_=t[:])
+            return t
+
+        def chunk_copy(c, t):
+            nc.scalar.copy(out=b12[:, D * c : D * (c + 1)], in_=t[:])
+
+        def bias_chunk(c, kb):
+            chunk_copy(c, chunk_mm(c, kb))
 
         o = {}
         outs = (out_1, out_2)
@@ -222,8 +234,7 @@ def tile_transformerblock_pa_w4_kernel(
             o[j] = sb.tile([P, D], F32, name="o%d" % j)
 
         def bias_of(j, n):
-            w, c = (j // 4) % 2, j % 4
-            return (b1_sb, b2_sb)[w][:, D * c + HALF * n : D * c + HALF * (n + 1)]
+            return b12[:, D * (j % 8) + HALF * n : D * (j % 8) + HALF * (n + 1)]
 
         def evac_v(j, n):
             nc.vector.tensor_tensor(out=o[j][:, sl[n]], in0=blk_ps[j][n][:], in1=bias_of(j, n), op=ADD)
@@ -242,37 +253,38 @@ def tile_transformerblock_pa_w4_kernel(
         def t_banks(ks, name):
             return [bank(ks[g], [P, 2, P], F32, "%s_%d" % (name, g)) for g in range(G)]
 
-        def do_xb(eng, b, n):
-            eng.tensor_tensor(out=xb[b][:, sl[n]], in0=xt[b][:, sl[n]], in1=bo_sb[:, sl[n]], op=ADD)
-
         warm = bank(3, [P, HALF], F32, "warm")
-        for i in range(6):
-            nc.tensor.matmul(warm[:], lhsT=zero[:, 0:P], rhs=zero[:], start=True, stop=True)
+        for i in range(2):
+            nc.tensor.matmul(warm[:], lhsT=ident_b[:], rhs=zero[:], start=True, stop=True)
         for b in range(B):
             nc.vector.tensor_copy(out=hbf[b][:, sl[0]], in_=hb[b][:, sl[0]].bitcast(FP8))
             nc.scalar.copy(out=hbf[b][:, sl[1]], in_=hb[b][:, sl[1]].bitcast(FP8))
-        for b in range(B):
-            for n in range(2):
-                do_xb(nc.gpsimd, b, n)
-        nc.gpsimd.memset(w2s[:].rearrange("p g n -> p (g n)").bitcast(I32), 0)
-        load_scales(w2s, w2_scales)
         hT[0] = t_banks((0, 1), "hT0")
         transposes(hT[0], hbf[0], (0, 1))
         hT[1] = t_banks((5, 6), "hT1")
         transposes(hT[1], hbf[1], (0, 1))
-        bias_chunk(0, 2)
-        bias_chunk(1, 7)
+        for n, kb in enumerate((2, 7)):
+            t = bank(kb, [P, HALF], F32, "xb_ps%d" % n)
+            nc.tensor.matmul(t[:], lhsT=ident_b[:], rhs=xt[0][:, sl[n]], start=True, stop=False)
+            nc.tensor.matmul(
+                t[:], lhsT=ident_b[:, 0:1].to_broadcast([P, P]), rhs=vrows[:, sl[n]], start=False, stop=True)
+            nc.scalar.copy(out=xb[0][:, sl[n]], in_=t[:])
         scale_rows(0, 0)
         scale_rows(0, 1)
         quant(codes[0], scal[0], qin[0], 0)
         quant(codes[0], scal[0], qin[0], 1)
         mm1(0, 3, 4)
+        for n in range(2):
+            t = bank(n, [P, HALF], BF16, "bo_ps%d" % n)
+            bcast_half(t, 0, n)
+            nc.scalar.copy(out=bo_sb[:, sl[n]], in_=t[:])
+            nc.gpsimd.tensor_tensor(out=xb[1][:, sl[n]], in0=bo_sb[:, sl[n]], in1=xt[1][:, sl[n]], op=ADD)
+        lng = bank(2, [P, D], BF16, "lng")
+        bcast(lng, 1)
+        lnb = bank(7, [P, D], BF16, "lnb")
+        bcast(lnb, 2)
         scale_rows(1, 0)
         scale_rows(1, 1)
-        lng = bank(0, [P, D], BF16, "lng")
-        bcast(lng, 1)
-        lnb = bank(1, [P, D], BF16, "lnb")
-        bcast(lnb, 2)
 
         do_y(0, 0)
         do_y(0, 1)
@@ -281,24 +293,27 @@ def tile_transformerblock_pa_w4_kernel(
         quant(codes[1], scal[1], qin[1], 1)
         rstd(rsy[0], ssy[0], y[0], nmy[0])
         mm1(1, 5, 6)
-        bias_chunk(2, 3)
-        fg = bank(2, [P, D], BF16, "fg")
+        bias_chunk(0, 3)
+        bias_chunk(1, 4)
+        fg = bank(0, [P, D], BF16, "fg")
         bcast(fg, 3)
+        fb = bank(1, [P, D], BF16, "fb")
+        bcast(fb, 4)
         do_u(0, 0)
         do_u(0, 1)
         do_y(1, 0)
         do_r(0, 0)
         do_r(0, 1)
-        bias_chunk(3, 4)
-        fb = bank(7, [P, D], BF16, "fb")
-        bcast(fb, 4)
         negmean(nmr[0], rsum[0])
         rstd(rsr[0], ssr[0], r[0], nmr[0])
         nc.sync.dma_start(out=out_r[0], in_=r[0][:])
         do_v(0, 0)
         do_v(0, 1)
+        bias_chunk(2, 3)
+        bias_chunk(5, 4)
         do_y(1, 1)
         negmean(nmy[1], ysum[1])
+        c3 = chunk_mm(3, 5)
         rstd(rsy[1], ssy[1], y[1], nmy[1])
         do_h(0, 0)
         do_h(0, 1)
@@ -308,15 +323,15 @@ def tile_transformerblock_pa_w4_kernel(
         evac_h(0, 0)
         transposes(h2T[0], h2[0], (1,))
         evac_h(0, 1)
-        warm2 = bank(5, [P, HALF], F32, "warm2")
-        for i in range(2):
-            nc.tensor.matmul(warm2[:], lhsT=zero[:, 0:P], rhs=zero[:], start=True, stop=True)
+        c4 = chunk_mm(4, 6)
+        chunk_copy(3, c3)
+        chunk_copy(4, c4)
         do_u(1, 0)
         quant(codes2[0], scal2[0], qin2[0], 0)
         do_u(1, 1)
         quant(codes2[0], scal2[0], qin2[0], 1)
 
-        mm2(0, (6, 5))
+        mm2(0, (3, 4))
         do_r(1, 0)
         do_r(1, 1)
         nc.sync.dma_start(out=out_r[1], in_=r[1][:])
@@ -325,10 +340,10 @@ def tile_transformerblock_pa_w4_kernel(
         negmean(nmr[1], rsum[1])
         evac_v(0, 1)
         store(0, 1)
-        mm2(1, (3, 4))
+        mm2(1, (5, 6))
         evac_s(1)
         rstd(rsr[1], ssr[1], r[1], nmr[1])
-        mm2(2, (6, 5))
+        mm2(2, (3, 4))
         do_v(1, 0)
         evac_v(2, 0)
         store(2, 0)
@@ -336,11 +351,11 @@ def tile_transformerblock_pa_w4_kernel(
         evac_v(2, 1)
         store(2, 1)
         store(1, 1)
-        mm2(3, (0, 1))
+        mm2(3, (5, 6))
         evac_s(3)
         do_v(1, 1)
         do_h(1, 0)
-        mm2(4, (3, 4))
+        mm2(4, (2, 7))
         evac_v(4, 0)
         evac_v(4, 1)
         store(4, 0)
@@ -348,9 +363,9 @@ def tile_transformerblock_pa_w4_kernel(
         store(4, 1)
         store(3, 1)
         do_h(1, 1)
-        mm2(5, (6, 5))
-        mm2(6, (0, 1))
-        h2T[1] = t_banks((2, 7), "h2T1")
+        mm2(5, (3, 4))
+        mm2(6, (5, 6))
+        h2T[1] = t_banks((0, 1), "h2T1")
         transposes(h2T[1], h2[1], (0, 1))
         evac_h(1, 0)
         evac_h(1, 1)
@@ -359,13 +374,13 @@ def tile_transformerblock_pa_w4_kernel(
         evac_v(5, 1)
         quant(codes2[1], scal2[1], qin2[1], 1)
         store(5)
-        mm2(7, (3, 4))
+        mm2(7, (2, 7))
         evac_s(6)
         evac_v(7, 0)
         evac_v(7, 1)
         store(7)
         plan = {8: "v", 9: "s", 10: "v", 11: "v", 12: "s", 13: "v", 14: "v", 15: "v"}
-        cyc = [(6, 5), (2, 7), (0, 1), (3, 4)]
+        cyc = [(3, 4), (0, 1), (5, 6), (2, 7)]
         late = [6]
         for i, j in enumerate(range(8, 16)):
             mm2(j, cyc[i % 4])

@@ -20,6 +20,7 @@ P = 128
 G = 2
 HALF = 512
 EPS = 1e-5
+NCH = 6
 
 FLOPS = 2 * B * T * D * (D + 2 * F)
 
@@ -64,42 +65,42 @@ def tile_transformerblock_pa_w4_kernel(
         hs = sb.tile([P, G, 4], F32, name="hs")
         xt = [sb.tile([P, D], BF16, name="xt%d" % b) for b in range(B)]
         wo = sb.tile([P, G, 2 * D], U8, name="wo", align_bytes=64)
-        wc = [[sb.tile([P, G, 2048], U8, name="w%d_%d" % (w, c), align_bytes=64) for c in range(4)] for w in range(2)]
-        b12 = sb.tile([P, 2 * F], BF16, name="b12")
+        wc = [sb.tile([P, G, 2 * F], U8, name="w%d" % w, align_bytes=64) for w in range(2)]
         bo_sb = sb.tile([P, D], BF16, name="bo_sb")
+        b12 = sb.tile([P, 2 * F], BF16, name="b12")
+        b2_rows = sb.tile([P, P], BF16, name="b2_rows")
+        b2_cols = sb.tile([P, 32], BF16, name="b2_cols")
+        nc.vector.memset(b2_rows[:].bitcast(I32), 0)
 
         def load_scales(dst, src):
             s32 = src.bitcast(I32).rearrange("g (q r) n -> r q g n", r=4)
             for r in range(4):
                 nc.sync.dma_start(out=dst[r:P:32, :, :].bitcast(I32), in_=s32[r])
 
-        def load_chunk(w, c):
-            src = (w1_words, w2_words)[w][:, :, 2048 * c : 2048 * (c + 1)].bitcast(I32)
-            nc.sync.dma_start(out=wc[w][c][:].bitcast(I32), in_=src.rearrange("g p n -> p g n"))
+        def load_words(w):
+            src = (w1_words, w2_words)[w].bitcast(I32)
+            nc.sync.dma_start(out=wc[w][:].bitcast(I32), in_=src.rearrange("g p n -> p g n"))
 
         nc.sync.dma_start(out=hb[0][:], in_=h_bytes[0])
         nc.scalar.dma_start(out=hs[:], in_=h_scale.rearrange("a o (g p t) -> p (a o g) t", p=P, t=4))
+        nc.scalar.dma_start(out=vrows[0:1, :], in_=bo.rearrange("(o c) -> o c", o=1))
         nc.scalar.activation(out=junk1[:], in_=one[:], func=ACT.Abs_reciprocal_sqrt, bias=EPS, scale=1.0)
         nc.sync.dma_start(out=hb[1][:], in_=h_bytes[1])
         nc.sync.dma_start(out=xt[0][:], in_=x[0])
-        for row, vec in enumerate((bo, ln2_g, ln2_b, fln_g, fln_b)):
+        nc.sync.dma_start(out=wo[:].bitcast(I32), in_=wo_words.bitcast(I32).rearrange("g p n -> p g n"))
+        for row, vec in enumerate((ln2_g, ln2_b, fln_g, fln_b), start=1):
             nc.scalar.dma_start(out=vrows[row : row + 1, :], in_=vec.rearrange("(o c) -> o c", o=1))
         nc.scalar.dma_start(out=vrows[5:9, :], in_=b1.rearrange("(r c) -> r c", r=4))
         nc.scalar.dma_start(out=vrows[9:11, :], in_=b2[0 : 2 * D].rearrange("(r c) -> r c", r=2))
+        nc.scalar.dma_start(out=b2_rows[0:32, :], in_=b2.rearrange("(r c) -> r c", r=32))
         load_scales(wos, wo_scales)
-        for g in range(G):
-            nc.sync.dma_start(out=wo[:, g, :].bitcast(I32), in_=wo_words[g].bitcast(I32))
         nc.sync.dma_start(out=xt[1][:], in_=x[1])
         load_scales(w1s, w1_scales)
-        for c in range(4):
-            load_chunk(0, c)
+        load_words(0)
         load_scales(w2s, w2_scales)
-        for c in range(4):
-            load_chunk(1, c)
-        nc.sync.dma_start(out=b12[:, 6 * D : 8 * D], in_=b2[2 * D : 4 * D].partition_broadcast(P))
+        load_words(1)
 
         hbf = [sb.tile([P, D], BF16, name="hbf%d" % b, align_bytes=64) for b in range(B)]
-        hT = [None, None]
         qin = [sb.tile([P, G, P, 4], BF16, name="qin%d" % b, align_bytes=64) for b in range(B)]
         codes = [sb.tile([P, G, P], U32, name="codes%d" % b, align_bytes=64) for b in range(B)]
         scal = [sb.tile([P, G, P], U8, name="scal%d" % b, align_bytes=64) for b in range(B)]
@@ -112,52 +113,8 @@ def tile_transformerblock_pa_w4_kernel(
         r = [sb.tile([P, D], F32, name="r%d" % b) for b in range(B)]
         v = [sb.tile([P, D], F32, name="v%d" % b) for b in range(B)]
         h2 = [sb.tile([P, D], BF16, name="h2_%d" % b, align_bytes=64) for b in range(B)]
-        sq = sb.tile([P, D], BF16, name="sq")
-        acc = [[None, None], [None, None]]
-        sl = [slice(0, HALF), slice(HALF, D)]
-
-        def transposes(dst, src, gs):
-            words = src[:].bitcast(F32)
-            for g in gs:
-                for k in range(2):
-                    nc.tensor.transpose(dst[g][:, k, :], words[:, 256 * g + k : 256 * (g + 1) : 2], ident_f[:])
-
-        def bcast(dst, row):
-            for i in range(2):
-                nc.tensor.matmul(
-                    dst[:, sl[i]], lhsT=ident_b[:, row : row + 1].to_broadcast([P, P]), rhs=vrows[:, sl[i]],
-                    start=True, stop=True,
-                )
-
-        def bcast_half(dst, row, n):
-            nc.tensor.matmul(
-                dst[:], lhsT=ident_b[:, row : row + 1].to_broadcast([P, P]), rhs=vrows[:, sl[n]],
-                start=True, stop=True,
-            )
-
-        def scale_rows(b, g):
-            src = hT[b][g][:].bitcast(BF16).rearrange("p k (n e) -> p n k e", e=2)
-            fac = hs[:, g, :].rearrange("p (k e) -> p k e", e=2).unsqueeze(1).to_broadcast([P, P, 2, 2])
-            nc.vector.tensor_tensor(
-                out=qin[b][:, g, :, :].rearrange("p n (k e) -> p n k e", e=2), in0=src, in1=fac, op=MULT
-            )
-
-        def quant(dst, sc, src, g):
-            nc.vector.quantize_mx(
-                out=dst[:, g, :].bitcast(FP8X4), scales=sc[:, g, :], in_=src[:, g, :, :].rearrange("p n t -> p (n t)")
-            )
-
-        def mm1(b, k0, k1):
-            for n, kb in enumerate((k0, k1)):
-                acc[b][n] = bank(kb, [P, HALF], F32, "acc%d_%d" % (b, n))
-                for g in range(G):
-                    nc.tensor.matmul_mx(
-                        out=acc[b][n][:],
-                        lhsT=codes[b][:, g, :].bitcast(FP8X4), lhsT_scale=scal[b][:, g, :],
-                        rhs=wo[:, g, 1024 * n : 1024 * (n + 1)].bitcast(FP4X4), rhs_scale=wos[:, g, sl[n]],
-                        start=(g == 0), stop=(g == G - 1),
-                    )
-
+        sq = [sb.tile([P, D], BF16, name="sq%d" % b) for b in range(B)]
+        o = [sb.tile([P, 2 * D], F32, name="o%d" % m) for m in range(8)]
         ysum = [st("ysum%d" % b, 2) for b in range(B)]
         rsum = [st("rsum%d" % b, 2) for b in range(B)]
         nmy = [st("nmy%d" % b) for b in range(B)]
@@ -166,233 +123,370 @@ def tile_transformerblock_pa_w4_kernel(
         ssr = [st("ssr%d" % b) for b in range(B)]
         rsy = [st("rsy%d" % b) for b in range(B)]
         rsr = [st("rsr%d" % b) for b in range(B)]
+        sl = [slice(0, HALF), slice(HALF, D)]
+        outs = (out_1, out_2)
+        pt = {}
+
+        def warm_mm(k):
+            pt["warm"] = bank(k, [P, HALF], F32, "warm")
+            for i in range(2):
+                nc.tensor.matmul(pt["warm"][:], lhsT=ident_b[:], rhs=zero[:], start=True, stop=True)
+
+        def cast_v(b, n):
+            nc.vector.tensor_copy(out=hbf[b][:, sl[n]], in_=hb[b][:, sl[n]].bitcast(FP8))
+
+        def cast_s(b, n):
+            nc.scalar.copy(out=hbf[b][:, sl[n]], in_=hb[b][:, sl[n]].bitcast(FP8))
+
+        def turn(kind, src, b, g, k):
+            t = bank(k, [P, 2, P], F32, "%s%d_%d" % (kind, b, g))
+            pt[kind, b, g] = t
+            words = src[b][:].bitcast(F32)
+            for e in range(2):
+                nc.tensor.transpose(t[:, e, :], words[:, 256 * g + e : 256 * (g + 1) : 2], ident_f[:])
+
+        def one_row(dst, row, cols, start=True):
+            nc.tensor.matmul(
+                dst, lhsT=ident_b[:, row : row + 1].to_broadcast([P, P]), rhs=vrows[:, cols], start=start, stop=True)
+
+        def resid_mm(b, n, k):
+            t = bank(k, [P, HALF], F32, "xb_ps%d_%d" % (b, n))
+            pt["xb", b, n] = t
+            nc.tensor.matmul(t[:], lhsT=ident_b[:], rhs=xt[b][:, sl[n]], start=True, stop=False)
+            one_row(t[:], 0, sl[n], start=False)
+
+        def resid_copy(b, n):
+            nc.scalar.copy(out=xb[b][:, sl[n]], in_=pt["xb", b, n][:])
+
+        def bo_mm(n, k):
+            pt["bo", n] = bank(k, [P, HALF], BF16, "bo_ps%d" % n)
+            one_row(pt["bo", n][:], 0, sl[n])
+
+        def bo_copy(n):
+            nc.scalar.copy(out=bo_sb[:, sl[n]], in_=pt["bo", n][:])
+
+        def xb_g(b, n):
+            nc.gpsimd.tensor_tensor(out=xb[b][:, sl[n]], in0=bo_sb[:, sl[n]], in1=xt[b][:, sl[n]], op=ADD)
+
+        def scale_rows(b, g):
+            src = pt["hT", b, g][:].bitcast(BF16).rearrange("p k (n e) -> p n k e", e=2)
+            fac = hs[:, g, :].rearrange("p (k e) -> p k e", e=2).unsqueeze(1).to_broadcast([P, P, 2, 2])
+            nc.vector.tensor_tensor(
+                out=qin[b][:, g, :, :].rearrange("p n (k e) -> p n k e", e=2), in0=src, in1=fac, op=MULT)
+
+        def quant(dst, sc, src, b, g):
+            nc.vector.quantize_mx(
+                out=dst[b][:, g, :].bitcast(FP8X4), scales=sc[b][:, g, :],
+                in_=src[b][:, g, :, :].rearrange("p n t -> p (n t)"))
+
+        def q1(b, g):
+            quant(codes, scal, qin, b, g)
+
+        def q2(b, g):
+            quant(codes2, scal2, qin2, b, g)
+
+        def mm1(b, n, k):
+            pt["acc", b, n] = bank(k, [P, HALF], F32, "acc%d_%d" % (b, n))
+            for g in range(G):
+                nc.tensor.matmul_mx(
+                    out=pt["acc", b, n][:],
+                    lhsT=codes[b][:, g, :].bitcast(FP8X4), lhsT_scale=scal[b][:, g, :],
+                    rhs=wo[:, g, 1024 * n : 1024 * (n + 1)].bitcast(FP4X4), rhs_scale=wos[:, g, sl[n]],
+                    start=(g == 0), stop=(g == G - 1))
+
+        def vec_mm(name, row, k):
+            pt[name] = bank(k, [P, D], BF16, name)
+            for n in range(2):
+                one_row(pt[name][:, sl[n]], row, sl[n])
 
         def do_y(b, n):
             nc.vector.scalar_tensor_tensor(
-                out=y[b][:, sl[n]], in0=acc[b][n][:], scalar=1.0, in1=xb[b][:, sl[n]], op0=MULT, op1=ADD,
-                accum_out=ysum[b][:, n : n + 1],
-            )
+                out=y[b][:, sl[n]], in0=pt["acc", b, n][:], scalar=1.0, in1=xb[b][:, sl[n]], op0=MULT, op1=ADD,
+                accum_out=ysum[b][:, n : n + 1])
 
-        def negmean(dst, sums):
-            nc.vector.tensor_scalar(out=dst[:], in0=sums[:, 0:1], scalar1=sums[:, 1:2], scalar2=-1.0 / D, op0=ADD, op1=MULT)
+        def negmean(dst, sums, b):
+            nc.vector.tensor_scalar(
+                out=dst[b][:], in0=sums[b][:, 0:1], scalar1=sums[b][:, 1:2], scalar2=-1.0 / D, op0=ADD, op1=MULT)
 
-        def rstd(dst, ss, src, nm):
-            nc.scalar.activation(out=sq[:], in_=src[:], func=ACT.Square, bias=nm[:], scale=1.0, accum_out=ss[:])
-            nc.scalar.activation(out=dst[:], in_=ss[:], func=ACT.Abs_reciprocal_sqrt, bias=EPS, scale=1.0 / D)
+        def nm_y(b):
+            negmean(nmy, ysum, b)
+
+        def nm_r(b):
+            negmean(nmr, rsum, b)
+
+        def sq_of(ss, src, nm, b):
+            nc.scalar.activation(
+                out=sq[b][:], in_=src[b][:], func=ACT.Square, bias=nm[b][:], scale=1.0, accum_out=ss[b][:])
+
+        def rs_of(dst, ss, b):
+            nc.scalar.activation(out=dst[b][:], in_=ss[b][:], func=ACT.Abs_reciprocal_sqrt, bias=EPS, scale=1.0 / D)
+
+        def sq_y(b):
+            sq_of(ssy, y, nmy, b)
+
+        def rs_y(b):
+            rs_of(rsy, ssy, b)
+
+        def sq_r(b):
+            sq_of(ssr, r, nmr, b)
+
+        def rs_r(b):
+            rs_of(rsr, ssr, b)
 
         def do_u(b, n):
             nc.vector.scalar_tensor_tensor(
-                out=u[b][:, sl[n]], in0=y[b][:, sl[n]], scalar=nmy[b][:], in1=lng[:, sl[n]], op0=ADD, op1=MULT)
+                out=u[b][:, sl[n]], in0=y[b][:, sl[n]], scalar=nmy[b][:], in1=pt["lng"][:, sl[n]], op0=ADD, op1=MULT)
 
         def do_r(b, n):
             nc.vector.scalar_tensor_tensor(
-                out=r[b][:, sl[n]], in0=u[b][:, sl[n]], scalar=rsy[b][:], in1=lnb[:, sl[n]], op0=MULT, op1=ADD,
+                out=r[b][:, sl[n]], in0=u[b][:, sl[n]], scalar=rsy[b][:], in1=pt["lnb"][:, sl[n]], op0=MULT, op1=ADD,
                 accum_out=rsum[b][:, n : n + 1])
 
         def do_v(b, n):
             nc.vector.scalar_tensor_tensor(
-                out=v[b][:, sl[n]], in0=r[b][:, sl[n]], scalar=nmr[b][:], in1=fg[:, sl[n]], op0=ADD, op1=MULT)
+                out=v[b][:, sl[n]], in0=r[b][:, sl[n]], scalar=nmr[b][:], in1=pt["fg"][:, sl[n]], op0=ADD, op1=MULT)
 
         def do_h(b, n):
             nc.vector.scalar_tensor_tensor(
-                out=h2[b][:, sl[n]], in0=v[b][:, sl[n]], scalar=rsr[b][:], in1=fb[:, sl[n]], op0=MULT, op1=ADD)
+                out=h2[b][:, sl[n]], in0=v[b][:, sl[n]], scalar=rsr[b][:], in1=pt["fb"][:, sl[n]], op0=MULT, op1=ADD)
 
         def evac_h(b, g):
             nc.scalar.copy(
                 out=qin2[b][:, g, :, :].rearrange("p n t -> p (n t)").bitcast(F32).rearrange("p (n k) -> p n k", k=2),
-                in_=h2T[b][g][:].rearrange("p k n -> p n k"))
+                in_=pt["h2T", b, g][:].rearrange("p k n -> p n k"))
 
-        def chunk_mm(c, kb):
-            t = bank(kb, [P, D], BF16, "bias%d" % c)
-            bcast(t, 5 + c)
-            return t
+        def b2_turn(k):
+            pt["b2t"] = bank(k, [P, P], BF16, "b2_t")
+            nc.tensor.transpose(pt["b2t"][:], b2_rows[:], ident_b[:])
 
-        def chunk_copy(c, t):
-            nc.scalar.copy(out=b12[:, D * c : D * (c + 1)], in_=t[:])
+        def b2_copy():
+            nc.scalar.copy(out=b2_cols[:], in_=pt["b2t"][:, 0:32])
 
-        def bias_chunk(c, kb):
-            chunk_copy(c, chunk_mm(c, kb))
+        def chunk_mm(c, k):
+            t = bank(k, [P, D], BF16, "bias%d" % c)
+            pt["bias", c] = t
+            if c < NCH:
+                for n in range(2):
+                    one_row(t[:, sl[n]], 5 + c, sl[n])
+            else:
+                for i in range(8):
+                    j = 8 * (c - 4) + i
+                    nc.tensor.transpose(t[:, P * i : P * (i + 1)], b2_cols[:, j : j + 1].to_broadcast([P, P]), ident_b[:])
 
-        o = {}
-        outs = (out_1, out_2)
-        blk_ps = {}
+        def chunk_copy(c):
+            nc.scalar.copy(out=b12[:, D * c : D * (c + 1)], in_=pt["bias", c][:])
 
-        def mm2(j, banks):
+        def mm2(j, k0, k1):
             b, w, c = j // 8, (j // 4) % 2, j % 4
             ws = (w1s, w2s)[w]
-            tiles = [bank(banks[n], [P, HALF], F32, "blk%d_%d" % (j, n)) for n in range(2)]
-            blk_ps[j] = tiles
+            for n in range(2):
+                pt["blk", j, n] = bank((k0, k1)[n], [P, HALF], F32, "blk%d_%d" % (j, n))
             for g in range(G):
                 for n in range(2):
+                    w0 = 2048 * c + 1024 * n
                     nc.tensor.matmul_mx(
-                        out=tiles[n][:],
+                        out=pt["blk", j, n][:],
                         lhsT=codes2[b][:, g, :].bitcast(FP8X4), lhsT_scale=scal2[b][:, g, :],
-                        rhs=wc[w][c][:, g, 1024 * n : 1024 * (n + 1)].bitcast(FP4X4),
+                        rhs=wc[w][:, g, w0 : w0 + 1024].bitcast(FP4X4),
                         rhs_scale=ws[:, g, D * c + HALF * n : D * c + HALF * (n + 1)],
-                        start=(g == 0), stop=(g == G - 1),
-                    )
-            o[j] = sb.tile([P, D], F32, name="o%d" % j)
+                        start=(g == 0), stop=(g == G - 1))
 
         def bias_of(j, n):
-            return b12[:, D * (j % 8) + HALF * n : D * (j % 8) + HALF * (n + 1)]
+            c0 = D * (j % 8) + HALF * n
+            return b12[:, c0 : c0 + HALF]
 
-        def evac_v(j, n):
-            nc.vector.tensor_tensor(out=o[j][:, sl[n]], in0=blk_ps[j][n][:], in1=bias_of(j, n), op=ADD)
+        def o_of(j, n):
+            c0 = D * (j % 2) + HALF * n
+            return o[j // 2][:, c0 : c0 + HALF]
 
-        def evac_s(j):
-            for n in range(2):
-                nc.scalar.copy(out=o[j][:, sl[n]], in_=blk_ps[j][n][:])
-            for n in range(2):
-                nc.gpsimd.tensor_tensor(out=o[j][:, sl[n]], in0=o[j][:, sl[n]], in1=bias_of(j, n), op=ADD)
+        def ev(j, n):
+            nc.vector.tensor_tensor(out=o_of(j, n), in0=pt["blk", j, n][:], in1=bias_of(j, n), op=ADD)
 
-        def store(j, n=None):
+        def es(j, n):
+            nc.scalar.copy(out=o_of(j, n), in_=pt["blk", j, n][:])
+
+        def eg(j, n):
+            nc.gpsimd.tensor_tensor(out=o_of(j, n), in0=o_of(j, n), in1=bias_of(j, n), op=ADD)
+
+        def put(j, n, width):
             b, w, c = j // 8, (j // 4) % 2, j % 4
-            cols = slice(0, D) if n is None else sl[n]
-            nc.sync.dma_start(out=outs[w][b, :, D * c + cols.start : D * c + cols.stop], in_=o[j][:, cols])
+            d0 = D * c + HALF * n
+            c0 = D * (j % 2) + HALF * n
+            nc.sync.dma_start(out=outs[w][b, :, d0 : d0 + width], in_=o[j // 2][:, c0 : c0 + width])
 
-        def t_banks(ks, name):
-            return [bank(ks[g], [P, 2, P], F32, "%s_%d" % (name, g)) for g in range(G)]
+        def store(j):
+            put(j, 0, D)
 
-        warm = bank(3, [P, HALF], F32, "warm")
-        for i in range(2):
-            nc.tensor.matmul(warm[:], lhsT=ident_b[:], rhs=zero[:], start=True, stop=True)
-        for b in range(B):
-            nc.vector.tensor_copy(out=hbf[b][:, sl[0]], in_=hb[b][:, sl[0]].bitcast(FP8))
-            nc.scalar.copy(out=hbf[b][:, sl[1]], in_=hb[b][:, sl[1]].bitcast(FP8))
-        hT[0] = t_banks((0, 1), "hT0")
-        transposes(hT[0], hbf[0], (0, 1))
-        hT[1] = t_banks((5, 6), "hT1")
-        transposes(hT[1], hbf[1], (0, 1))
-        for n, kb in enumerate((2, 7)):
-            t = bank(kb, [P, HALF], F32, "xb_ps%d" % n)
-            nc.tensor.matmul(t[:], lhsT=ident_b[:], rhs=xt[0][:, sl[n]], start=True, stop=False)
-            nc.tensor.matmul(
-                t[:], lhsT=ident_b[:, 0:1].to_broadcast([P, P]), rhs=vrows[:, sl[n]], start=False, stop=True)
-            nc.scalar.copy(out=xb[0][:, sl[n]], in_=t[:])
+        def store_half(j, n):
+            put(j, n, HALF)
+
+        def store_two(j):
+            put(j, 0, 2 * D)
+
+        def store_r(b):
+            nc.sync.dma_start(out=out_r[b], in_=r[b][:])
+
+        cast_s(0, 1)
+        warm_mm(7)
+        cast_v(0, 0)
+        turn("hT", hbf, 0, 0, 1)
+        cast_s(1, 1)
+        turn("hT", hbf, 0, 1, 6)
+        cast_v(1, 0)
+        resid_mm(0, 1, 2)
         scale_rows(0, 0)
+        turn("hT", hbf, 1, 1, 4)
         scale_rows(0, 1)
-        quant(codes[0], scal[0], qin[0], 0)
-        quant(codes[0], scal[0], qin[0], 1)
-        mm1(0, 3, 4)
-        for n in range(2):
-            t = bank(n, [P, HALF], BF16, "bo_ps%d" % n)
-            bcast_half(t, 0, n)
-            nc.scalar.copy(out=bo_sb[:, sl[n]], in_=t[:])
-            nc.gpsimd.tensor_tensor(out=xb[1][:, sl[n]], in0=bo_sb[:, sl[n]], in1=xt[1][:, sl[n]], op=ADD)
-        lng = bank(2, [P, D], BF16, "lng")
-        bcast(lng, 1)
-        lnb = bank(7, [P, D], BF16, "lnb")
-        bcast(lnb, 2)
-        scale_rows(1, 0)
+        turn("hT", hbf, 1, 0, 5)
+        q1(0, 0)
+        resid_copy(0, 1)
+        resid_mm(0, 0, 3)
+        bo_mm(0, 7)
+        q1(0, 1)
+        mm1(0, 0, 6)
         scale_rows(1, 1)
-
+        scale_rows(1, 0)
+        resid_copy(0, 0)
+        mm1(0, 1, 4)
+        q1(1, 1)
         do_y(0, 0)
+        bo_copy(0)
+        bo_mm(1, 0)
+        bo_copy(1)
+        xb_g(1, 1)
+        chunk_mm(2, 3)
         do_y(0, 1)
-        quant(codes[1], scal[1], qin[1], 0)
-        negmean(nmy[0], ysum[0])
-        quant(codes[1], scal[1], qin[1], 1)
-        rstd(rsy[0], ssy[0], y[0], nmy[0])
-        mm1(1, 5, 6)
-        bias_chunk(0, 3)
-        bias_chunk(1, 4)
-        fg = bank(0, [P, D], BF16, "fg")
-        bcast(fg, 3)
-        fb = bank(1, [P, D], BF16, "fb")
-        bcast(fb, 4)
+        vec_mm("lng", 1, 2)
+        chunk_mm(1, 7)
+        chunk_copy(2)
+        q1(1, 0)
+        nm_y(0)
+        mm1(1, 1, 0)
+        vec_mm("lnb", 2, 4)
+        chunk_mm(0, 3)
+        sq_y(0)
         do_u(0, 0)
+        xb_g(1, 0)
+        chunk_mm(3, 5)
+        rs_y(0)
         do_u(0, 1)
-        do_y(1, 0)
-        do_r(0, 0)
-        do_r(0, 1)
-        negmean(nmr[0], rsum[0])
-        rstd(rsr[0], ssr[0], r[0], nmr[0])
-        nc.sync.dma_start(out=out_r[0], in_=r[0][:])
-        do_v(0, 0)
-        do_v(0, 1)
-        bias_chunk(2, 3)
-        bias_chunk(5, 4)
+        chunk_copy(1)
         do_y(1, 1)
-        negmean(nmy[1], ysum[1])
-        c3 = chunk_mm(3, 5)
-        rstd(rsy[1], ssy[1], y[1], nmy[1])
-        do_h(0, 0)
-        do_h(0, 1)
-        h2T = [None, None]
-        h2T[0] = t_banks((3, 4), "h2T0")
-        transposes(h2T[0], h2[0], (0,))
-        evac_h(0, 0)
-        transposes(h2T[0], h2[0], (1,))
-        evac_h(0, 1)
-        c4 = chunk_mm(4, 6)
-        chunk_copy(3, c3)
-        chunk_copy(4, c4)
-        do_u(1, 0)
-        quant(codes2[0], scal2[0], qin2[0], 0)
+        mm1(1, 0, 7)
+        vec_mm("fg", 3, 1)
+        chunk_copy(0)
+        do_r(0, 1)
+        chunk_copy(3)
+        do_r(0, 0)
+        nm_r(0)
+        sq_r(0)
+        do_y(1, 0)
+        b2_turn(3)
+        b2_copy()
+        vec_mm("fb", 4, 7)
+        do_v(0, 1)
+        chunk_mm(5, 3)
+        nm_y(1)
+        rs_r(0)
+        sq_y(1)
+        chunk_copy(5)
+        do_v(0, 0)
         do_u(1, 1)
-        quant(codes2[0], scal2[0], qin2[0], 1)
-
-        mm2(0, (3, 4))
-        do_r(1, 0)
+        rs_y(1)
+        do_h(0, 0)
+        chunk_mm(6, 0)
+        do_h(0, 1)
+        turn("h2T", h2, 0, 0, 5)
+        turn("h2T", h2, 0, 1, 6)
+        do_u(1, 0)
+        evac_h(0, 0)
         do_r(1, 1)
-        nc.sync.dma_start(out=out_r[1], in_=r[1][:])
-        evac_v(0, 0)
-        store(0, 0)
-        negmean(nmr[1], rsum[1])
-        evac_v(0, 1)
-        store(0, 1)
-        mm2(1, (5, 6))
-        evac_s(1)
-        rstd(rsr[1], ssr[1], r[1], nmr[1])
-        mm2(2, (3, 4))
-        do_v(1, 0)
-        evac_v(2, 0)
-        store(2, 0)
-        store(1, 0)
-        evac_v(2, 1)
-        store(2, 1)
-        store(1, 1)
-        mm2(3, (5, 6))
-        evac_s(3)
+        evac_h(0, 1)
+        chunk_mm(4, 3)
+        q2(0, 0)
+        q2(0, 1)
+        chunk_copy(6)
+        mm2(0, 5, 6)
+        do_r(1, 0)
+        nm_r(1)
+        ev(0, 0)
+        chunk_copy(4)
+        store_r(0)
+        sq_r(1)
         do_v(1, 1)
-        do_h(1, 0)
-        mm2(4, (2, 7))
-        evac_v(4, 0)
-        evac_v(4, 1)
-        store(4, 0)
-        store(3, 0)
-        store(4, 1)
-        store(3, 1)
+        mm2(1, 4, 3)
+        mm2(3, 5, 0)
+        es(1, 0)
+        do_v(1, 0)
+        store_r(1)
+        rs_r(1)
+        ev(0, 1)
+        ev(1, 1)
+        mm2(6, 2, 4)
         do_h(1, 1)
-        mm2(5, (3, 4))
-        mm2(6, (5, 6))
-        h2T[1] = t_banks((0, 1), "h2T1")
-        transposes(h2T[1], h2[1], (0, 1))
-        evac_h(1, 0)
+        do_h(1, 0)
+        es(3, 1)
+        mm2(2, 1, 3)
+        es(3, 0)
+        turn("h2T", h2, 1, 0, 7)
+        turn("h2T", h2, 1, 1, 5)
+        ev(6, 0)
+        ev(6, 1)
         evac_h(1, 1)
-        evac_v(5, 0)
-        quant(codes2[1], scal2[1], qin2[1], 0)
-        evac_v(5, 1)
-        quant(codes2[1], scal2[1], qin2[1], 1)
-        store(5)
-        mm2(7, (2, 7))
-        evac_s(6)
-        evac_v(7, 0)
-        evac_v(7, 1)
+        store_half(0, 0)
+        ev(2, 1)
+        mm2(4, 6, 2)
+        ev(2, 0)
+        q2(1, 1)
+        evac_h(1, 0)
+        q2(1, 0)
+        ev(4, 0)
+        mm2(5, 3, 5)
+        es(4, 1)
+        ev(5, 0)
+        eg(1, 0)
+        mm2(9, 1, 4)
+        ev(5, 1)
+        ev(9, 0)
+        store_half(0, 1)
+        ev(9, 1)
+        mm2(8, 6, 0)
+        ev(8, 0)
+        mm2(10, 5, 1)
+        mm2(11, 7, 4)
+        store(1)
+        ev(8, 1)
+        ev(10, 1)
+        chunk_mm(7, 6)
+        mm2(7, 0, 3)
+        eg(3, 1)
+        eg(3, 0)
+        store(6)
+        ev(10, 0)
+        mm2(15, 5, 2)
+        chunk_copy(7)
+        ev(11, 0)
+        es(15, 0)
+        ev(11, 1)
+        ev(7, 0)
+        mm2(14, 0, 4)
+        eg(4, 1)
+        ev(7, 1)
+        ev(15, 1)
+        store_two(2)
+        mm2(12, 1, 2)
+        ev(14, 0)
+        store_two(4)
+        eg(15, 0)
+        ev(14, 1)
+        store_two(8)
+        mm2(13, 6, 3)
+        ev(12, 1)
+        store_two(10)
+        es(12, 0)
+        ev(13, 0)
+        ev(13, 1)
+        eg(12, 0)
         store(7)
-        plan = {8: "v", 9: "s", 10: "v", 11: "v", 12: "s", 13: "v", 14: "v", 15: "v"}
-        cyc = [(3, 4), (0, 1), (5, 6), (2, 7)]
-        late = [6]
-        for i, j in enumerate(range(8, 16)):
-            mm2(j, cyc[i % 4])
-            if plan[j] == "s":
-                evac_s(j)
-                late.append(j)
-            else:
-                for n in range(2):
-                    evac_v(j, n)
-                    if j >= 14:
-                        store(j, n)
-                if j < 14:
-                    store(j)
-                if late and j != 10 and j != 13:
-                    store(late.pop(0))
+        store_two(14)
+        store_two(12)

@@ -17,10 +17,9 @@ ACT = mybir.ActivationFunctionType
 
 B, T, D, F = 2, 128, 1024, 4096
 P = 128
-G = 2
+G = D // 512
 HALF = 512
 EPS = 1e-5
-NCH = 6
 
 FLOPS = 2 * B * T * D * (D + 2 * F)
 
@@ -38,105 +37,104 @@ def tile_transformerblock_pa_w4_kernel(
         def bank(i, shape, dtype, name):
             return ps.tile(shape, dtype, tag="bank%d" % i, name=name)
 
-        def st(name, w=1):
-            return sb.tile([P, w], F32, name=name)
+        def pair(shape, dtype, name):
+            return [sb.tile(shape, dtype, name="%s%d" % (name, b), align_bytes=64) for b in range(B)]
 
         vrows = sb.tile([P, D], BF16, name="vrows")
-        wos = sb.tile([P, G, D], U8, name="wos", align_bytes=64)
-        w1s = sb.tile([P, G, F], U8, name="w1s", align_bytes=64)
-        w2s = sb.tile([P, G, F], U8, name="w2s", align_bytes=64)
+        b1_rows = sb.tile([P, P], BF16, name="b1_rows")
+        b1_cols = sb.tile([P, 32], BF16, name="b1_cols")
         ident_f = sb.tile([P, P], F32, name="ident_f")
         ident_b = sb.tile([P, P], BF16, name="ident_b")
         zero = sb.tile([P, HALF], BF16, name="zero")
-        one = st("one")
-        junk1 = st("junk1")
+        one = sb.tile([P, 1], F32, name="one")
+        one_out = sb.tile([P, 1], F32, name="one_out")
+        wos = sb.tile([P, G, D], U8, name="wos", align_bytes=64)
+        w1s = sb.tile([P, G, F], U8, name="w1s", align_bytes=64)
 
         nc.gpsimd.memset(vrows[:].bitcast(I32), 0)
-        nc.vector.memset(wos[:].rearrange("p g n -> p (g n)").bitcast(I32), 0)
-        nc.vector.memset(one[:], 1.0)
-        nc.vector.memset(zero[:].bitcast(I32), 0)
         make_identity(nc, ident_f[:])
-        make_identity(nc, ident_b[:])
+        nc.vector.memset(zero[:].bitcast(I32), 0)
+        nc.vector.memset(one[:], 1.0)
+        nc.vector.memset(wos[:].bitcast(I32), 0)
+        nc.vector.memset(b1_rows[:].bitcast(I32), 0)
+        nc.vector.tensor_copy(out=ident_b[:], in_=ident_f[:])
         nc.vector.memset(w1s[:, 0, :].bitcast(I32), 0)
-        nc.gpsimd.memset(w1s[:, 1, :].bitcast(I32), 0)
-        nc.gpsimd.memset(w2s[:].rearrange("p g n -> p (g n)").bitcast(I32), 0)
 
-        hb = [sb.tile([P, D], U8, name="hb%d" % b, align_bytes=64) for b in range(B)]
+        hb = pair([P, D], U8, "hb")
+        xt = pair([P, D], BF16, "xt")
         hs = sb.tile([P, G, 4], F32, name="hs")
-        xt = [sb.tile([P, D], BF16, name="xt%d" % b) for b in range(B)]
         wo = sb.tile([P, G, 2 * D], U8, name="wo", align_bytes=64)
-        wc = [sb.tile([P, G, 2 * F], U8, name="w%d" % w, align_bytes=64) for w in range(2)]
-        bo_sb = sb.tile([P, D], BF16, name="bo_sb")
+        wc = pair([P, G, 2 * F], U8, "wc")
         b12 = sb.tile([P, 2 * F], BF16, name="b12")
-        b2_rows = sb.tile([P, P], BF16, name="b2_rows")
-        b2_cols = sb.tile([P, 32], BF16, name="b2_cols")
-        nc.vector.memset(b2_rows[:].bitcast(I32), 0)
+
+        def load_words(dst, src):
+            nc.sync.dma_start(out=dst[:].bitcast(I32), in_=src.bitcast(I32).rearrange("g p n -> p g n"))
 
         def load_scales(dst, src):
-            s32 = src.bitcast(I32).rearrange("g (q r) n -> r q g n", r=4)
+            words = src.bitcast(I32).rearrange("g (q r) n -> r q g n", r=4)
             for r in range(4):
-                nc.sync.dma_start(out=dst[r:P:32, :, :].bitcast(I32), in_=s32[r])
+                nc.sync.dma_start(out=dst[r:P:32, :, :].bitcast(I32), in_=words[r])
 
-        def load_words(w):
-            src = (w1_words, w2_words)[w].bitcast(I32)
-            nc.sync.dma_start(out=wc[w][:].bitcast(I32), in_=src.rearrange("g p n -> p g n"))
+        def load_row(dst, vec):
+            nc.scalar.dma_start(out=dst, in_=vec.rearrange("(o c) -> o c", o=1))
 
         nc.sync.dma_start(out=hb[0][:], in_=h_bytes[0])
         nc.scalar.dma_start(out=hs[:], in_=h_scale.rearrange("a o (g p t) -> p (a o g) t", p=P, t=4))
-        nc.scalar.dma_start(out=vrows[0:1, :], in_=bo.rearrange("(o c) -> o c", o=1))
-        nc.scalar.activation(out=junk1[:], in_=one[:], func=ACT.Abs_reciprocal_sqrt, bias=EPS, scale=1.0)
+        load_row(vrows[0:1, :], bo)
         nc.sync.dma_start(out=hb[1][:], in_=h_bytes[1])
         nc.sync.dma_start(out=xt[0][:], in_=x[0])
-        nc.sync.dma_start(out=wo[:].bitcast(I32), in_=wo_words.bitcast(I32).rearrange("g p n -> p g n"))
-        for row, vec in enumerate((ln2_g, ln2_b, fln_g, fln_b), start=1):
-            nc.scalar.dma_start(out=vrows[row : row + 1, :], in_=vec.rearrange("(o c) -> o c", o=1))
-        nc.scalar.dma_start(out=vrows[5:9, :], in_=b1.rearrange("(r c) -> r c", r=4))
-        nc.scalar.dma_start(out=vrows[9:11, :], in_=b2[0 : 2 * D].rearrange("(r c) -> r c", r=2))
-        nc.scalar.dma_start(out=b2_rows[0:32, :], in_=b2.rearrange("(r c) -> r c", r=32))
+        load_words(wo, wo_words)
+        for i, vec in enumerate((ln2_g, ln2_b, fln_g, fln_b), start=1):
+            load_row(vrows[i : i + 1, :], vec)
+        nc.scalar.dma_start(out=vrows[5:9, :], in_=b2.rearrange("(r c) -> r c", r=4))
+        nc.scalar.dma_start(out=b1_rows[0:32, :], in_=b1.rearrange("(r c) -> r c", r=32))
+        nc.scalar.activation(out=one_out[:], in_=one[:], func=ACT.Abs_reciprocal_sqrt, bias=EPS, scale=1.0)
         load_scales(wos, wo_scales)
         nc.sync.dma_start(out=xt[1][:], in_=x[1])
-        load_scales(w1s, w1_scales)
-        load_words(0)
-        load_scales(w2s, w2_scales)
-        load_words(1)
 
-        hbf = [sb.tile([P, D], BF16, name="hbf%d" % b, align_bytes=64) for b in range(B)]
-        qin = [sb.tile([P, G, P, 4], BF16, name="qin%d" % b, align_bytes=64) for b in range(B)]
-        codes = [sb.tile([P, G, P], U32, name="codes%d" % b, align_bytes=64) for b in range(B)]
-        scal = [sb.tile([P, G, P], U8, name="scal%d" % b, align_bytes=64) for b in range(B)]
-        qin2 = [sb.tile([P, G, P, 4], BF16, name="qin2_%d" % b, align_bytes=64) for b in range(B)]
-        codes2 = [sb.tile([P, G, P], U32, name="codes2_%d" % b, align_bytes=64) for b in range(B)]
-        scal2 = [sb.tile([P, G, P], U8, name="scal2_%d" % b, align_bytes=64) for b in range(B)]
-        xb = [sb.tile([P, D], F32, name="xb%d" % b) for b in range(B)]
-        y = [sb.tile([P, D], F32, name="y%d" % b) for b in range(B)]
-        u = [sb.tile([P, D], F32, name="u%d" % b) for b in range(B)]
-        r = [sb.tile([P, D], F32, name="r%d" % b) for b in range(B)]
-        v = [sb.tile([P, D], F32, name="v%d" % b) for b in range(B)]
-        h2 = [sb.tile([P, D], BF16, name="h2_%d" % b, align_bytes=64) for b in range(B)]
-        sq = [sb.tile([P, D], BF16, name="sq%d" % b) for b in range(B)]
+        hbf = pair([P, D], BF16, "hbf")
+        qin = [
+            sb.tile([P, G, P, 4], BF16, name="qin%d" % b, tag=("qin0", "qin1_then_w2s")[b], align_bytes=64)
+            for b in range(B)
+        ]
+        codes = pair([P, G, P], U32, "codes")
+        scal = pair([P, G, P], U8, "scal")
+        qin2 = pair([P, G, P, 4], BF16, "qin2_")
+        codes2 = pair([P, G, P], U32, "codes2_")
+        scal2 = pair([P, G, P], U8, "scal2_")
+        xb = pair([P, D], F32, "xb")
+        y = pair([P, D], F32, "y")
+        u = pair([P, D], F32, "u")
+        r = pair([P, D], F32, "r")
+        v = pair([P, D], F32, "v")
+        h2 = pair([P, D], BF16, "h2_")
+        sq = pair([P, D], BF16, "sq")
         o = [sb.tile([P, 2 * D], F32, name="o%d" % m) for m in range(8)]
-        ysum = [st("ysum%d" % b, 2) for b in range(B)]
-        rsum = [st("rsum%d" % b, 2) for b in range(B)]
-        nmy = [st("nmy%d" % b) for b in range(B)]
-        nmr = [st("nmr%d" % b) for b in range(B)]
-        ssy = [st("ssy%d" % b) for b in range(B)]
-        ssr = [st("ssr%d" % b) for b in range(B)]
-        rsy = [st("rsy%d" % b) for b in range(B)]
-        rsr = [st("rsr%d" % b) for b in range(B)]
+
+        ysum, rsum = pair([P, 2], F32, "ysum"), pair([P, 2], F32, "rsum")
+        nmy, nmr = pair([P, 1], F32, "nmy"), pair([P, 1], F32, "nmr")
+        ssy, ssr = pair([P, 1], F32, "ssy"), pair([P, 1], F32, "ssr")
+        rsy, rsr = pair([P, 1], F32, "rsy"), pair([P, 1], F32, "rsr")
+
         sl = [slice(0, HALF), slice(HALF, D)]
         outs = (out_1, out_2)
         pt = {}
+        w2s = {}
 
-        def warm_mm(k):
-            pt["warm"] = bank(k, [P, HALF], F32, "warm")
-            for i in range(2):
-                nc.tensor.matmul(pt["warm"][:], lhsT=ident_b[:], rhs=zero[:], start=True, stop=True)
+        def spin(k):
+            pt["spin"] = bank(k, [P, HALF], F32, "spin")
+            for _ in range(4):
+                nc.tensor.matmul(pt["spin"][:], lhsT=zero[:, 0:P], rhs=zero[:], start=True, stop=True)
 
-        def cast_v(b, n):
-            nc.vector.tensor_copy(out=hbf[b][:, sl[n]], in_=hb[b][:, sl[n]].bitcast(FP8))
+        def zero_w1s():
+            nc.vector.memset(w1s[:, 1, :].bitcast(I32), 0)
 
-        def cast_s(b, n):
-            nc.scalar.copy(out=hbf[b][:, sl[n]], in_=hb[b][:, sl[n]].bitcast(FP8))
+        def zero_w2s():
+            w2s["t"] = sb.tile([P, G, F], U8, name="w2s", tag="qin1_then_w2s", align_bytes=64)
+            nc.gpsimd.memset(w2s["t"][:].bitcast(I32), 0)
+
+        def cast(copy, b, n):
+            copy(out=hbf[b][:, sl[n]], in_=hb[b][:, sl[n]].bitcast(FP8))
 
         def turn(kind, src, b, g, k):
             t = bank(k, [P, 2, P], F32, "%s%d_%d" % (kind, b, g))
@@ -145,28 +143,18 @@ def tile_transformerblock_pa_w4_kernel(
             for e in range(2):
                 nc.tensor.transpose(t[:, e, :], words[:, 256 * g + e : 256 * (g + 1) : 2], ident_f[:])
 
-        def one_row(dst, row, cols, start=True):
+        def add_row(dst, row, cols, start=True):
             nc.tensor.matmul(
                 dst, lhsT=ident_b[:, row : row + 1].to_broadcast([P, P]), rhs=vrows[:, cols], start=start, stop=True)
 
-        def resid_mm(b, n, k):
+        def x_plus_bo(b, n, k):
             t = bank(k, [P, HALF], F32, "xb_ps%d_%d" % (b, n))
             pt["xb", b, n] = t
             nc.tensor.matmul(t[:], lhsT=ident_b[:], rhs=xt[b][:, sl[n]], start=True, stop=False)
-            one_row(t[:], 0, sl[n], start=False)
+            add_row(t[:], 0, sl[n], start=False)
 
-        def resid_copy(b, n):
+        def keep_xb(b, n):
             nc.scalar.copy(out=xb[b][:, sl[n]], in_=pt["xb", b, n][:])
-
-        def bo_mm(n, k):
-            pt["bo", n] = bank(k, [P, HALF], BF16, "bo_ps%d" % n)
-            one_row(pt["bo", n][:], 0, sl[n])
-
-        def bo_copy(n):
-            nc.scalar.copy(out=bo_sb[:, sl[n]], in_=pt["bo", n][:])
-
-        def xb_g(b, n):
-            nc.gpsimd.tensor_tensor(out=xb[b][:, sl[n]], in0=bo_sb[:, sl[n]], in1=xt[b][:, sl[n]], op=ADD)
 
         def scale_rows(b, g):
             src = pt["hT", b, g][:].bitcast(BF16).rearrange("p k (n e) -> p n k e", e=2)
@@ -174,319 +162,300 @@ def tile_transformerblock_pa_w4_kernel(
             nc.vector.tensor_tensor(
                 out=qin[b][:, g, :, :].rearrange("p n (k e) -> p n k e", e=2), in0=src, in1=fac, op=MULT)
 
-        def quant(dst, sc, src, b, g):
+        def quantise(dst, scales, src, g):
             nc.vector.quantize_mx(
-                out=dst[b][:, g, :].bitcast(FP8X4), scales=sc[b][:, g, :],
-                in_=src[b][:, g, :, :].rearrange("p n t -> p (n t)"))
+                out=dst[:, g, :].bitcast(FP8X4), scales=scales[:, g, :],
+                in_=src[:, g, :, :].rearrange("p n t -> p (n t)"))
 
-        def q1(b, g):
-            quant(codes, scal, qin, b, g)
+        def q_h(b, g):
+            quantise(codes[b], scal[b], qin[b], g)
 
-        def q2(b, g):
-            quant(codes2, scal2, qin2, b, g)
+        def q_h2(b, g):
+            quantise(codes2[b], scal2[b], qin2[b], g)
 
-        def mm1(b, n, k):
+        def mm_wo(b, n, k):
             pt["acc", b, n] = bank(k, [P, HALF], F32, "acc%d_%d" % (b, n))
             for g in range(G):
                 nc.tensor.matmul_mx(
                     out=pt["acc", b, n][:],
                     lhsT=codes[b][:, g, :].bitcast(FP8X4), lhsT_scale=scal[b][:, g, :],
-                    rhs=wo[:, g, 1024 * n : 1024 * (n + 1)].bitcast(FP4X4), rhs_scale=wos[:, g, sl[n]],
+                    rhs=wo[:, g, 2 * HALF * n : 2 * HALF * (n + 1)].bitcast(FP4X4), rhs_scale=wos[:, g, sl[n]],
                     start=(g == 0), stop=(g == G - 1))
 
-        def vec_mm(name, row, k):
+        def spread(name, row, k):
             pt[name] = bank(k, [P, D], BF16, name)
             for n in range(2):
-                one_row(pt[name][:, sl[n]], row, sl[n])
+                add_row(pt[name][:, sl[n]], row, sl[n])
 
         def do_y(b, n):
             nc.vector.scalar_tensor_tensor(
                 out=y[b][:, sl[n]], in0=pt["acc", b, n][:], scalar=1.0, in1=xb[b][:, sl[n]], op0=MULT, op1=ADD,
                 accum_out=ysum[b][:, n : n + 1])
 
-        def negmean(dst, sums, b):
+        def negmean(dst, sums):
             nc.vector.tensor_scalar(
-                out=dst[b][:], in0=sums[b][:, 0:1], scalar1=sums[b][:, 1:2], scalar2=-1.0 / D, op0=ADD, op1=MULT)
+                out=dst[:], in0=sums[:, 0:1], scalar1=sums[:, 1:2], scalar2=-1.0 / D, op0=ADD, op1=MULT)
 
-        def nm_y(b):
-            negmean(nmy, ysum, b)
-
-        def nm_r(b):
-            negmean(nmr, rsum, b)
-
-        def sq_of(ss, src, nm, b):
+        def squares(total, src, nm, b):
             nc.scalar.activation(
-                out=sq[b][:], in_=src[b][:], func=ACT.Square, bias=nm[b][:], scale=1.0, accum_out=ss[b][:])
+                out=sq[b][:], in_=src[b][:], func=ACT.Square, bias=nm[b][:], scale=1.0, accum_out=total[b][:])
 
-        def rs_of(dst, ss, b):
-            nc.scalar.activation(out=dst[b][:], in_=ss[b][:], func=ACT.Abs_reciprocal_sqrt, bias=EPS, scale=1.0 / D)
+        def rstd(dst, total):
+            nc.scalar.activation(out=dst[:], in_=total[:], func=ACT.Abs_reciprocal_sqrt, bias=EPS, scale=1.0 / D)
 
-        def sq_y(b):
-            sq_of(ssy, y, nmy, b)
-
-        def rs_y(b):
-            rs_of(rsy, ssy, b)
-
-        def sq_r(b):
-            sq_of(ssr, r, nmr, b)
-
-        def rs_r(b):
-            rs_of(rsr, ssr, b)
+        def centre(dst, src, nm, gain, b, n):
+            nc.vector.scalar_tensor_tensor(
+                out=dst[b][:, sl[n]], in0=src[b][:, sl[n]], scalar=nm[b][:], in1=pt[gain][:, sl[n]], op0=ADD, op1=MULT)
 
         def do_u(b, n):
-            nc.vector.scalar_tensor_tensor(
-                out=u[b][:, sl[n]], in0=y[b][:, sl[n]], scalar=nmy[b][:], in1=pt["lng"][:, sl[n]], op0=ADD, op1=MULT)
+            centre(u, y, nmy, "ln2_g", b, n)
+
+        def do_v(b, n):
+            centre(v, r, nmr, "fln_g", b, n)
 
         def do_r(b, n):
             nc.vector.scalar_tensor_tensor(
-                out=r[b][:, sl[n]], in0=u[b][:, sl[n]], scalar=rsy[b][:], in1=pt["lnb"][:, sl[n]], op0=MULT, op1=ADD,
+                out=r[b][:, sl[n]], in0=u[b][:, sl[n]], scalar=rsy[b][:], in1=pt["ln2_b"][:, sl[n]], op0=MULT, op1=ADD,
                 accum_out=rsum[b][:, n : n + 1])
 
-        def do_v(b, n):
+        def do_h2(b, n):
             nc.vector.scalar_tensor_tensor(
-                out=v[b][:, sl[n]], in0=r[b][:, sl[n]], scalar=nmr[b][:], in1=pt["fg"][:, sl[n]], op0=ADD, op1=MULT)
+                out=h2[b][:, sl[n]], in0=v[b][:, sl[n]], scalar=rsr[b][:], in1=pt["fln_b"][:, sl[n]], op0=MULT, op1=ADD)
 
-        def do_h(b, n):
-            nc.vector.scalar_tensor_tensor(
-                out=h2[b][:, sl[n]], in0=v[b][:, sl[n]], scalar=rsr[b][:], in1=pt["fb"][:, sl[n]], op0=MULT, op1=ADD)
-
-        def evac_h(b, g):
-            nc.scalar.copy(
+        def lay_h2(copy, b, g):
+            copy(
                 out=qin2[b][:, g, :, :].rearrange("p n t -> p (n t)").bitcast(F32).rearrange("p (n k) -> p n k", k=2),
                 in_=pt["h2T", b, g][:].rearrange("p k n -> p n k"))
 
-        def b2_turn(k):
-            pt["b2t"] = bank(k, [P, P], BF16, "b2_t")
-            nc.tensor.transpose(pt["b2t"][:], b2_rows[:], ident_b[:])
+        def b1_turn(k):
+            pt["b1"] = bank(k, [P, P], BF16, "b1_t")
+            nc.tensor.transpose(pt["b1"][:], b1_rows[:], ident_b[:])
 
-        def b2_copy():
-            nc.scalar.copy(out=b2_cols[:], in_=pt["b2t"][:, 0:32])
-
-        def chunk_mm(c, k):
+        def bias(c, k):
             t = bank(k, [P, D], BF16, "bias%d" % c)
             pt["bias", c] = t
-            if c < NCH:
-                for n in range(2):
-                    one_row(t[:, sl[n]], 5 + c, sl[n])
-            else:
+            if c < 4:
                 for i in range(8):
-                    j = 8 * (c - 4) + i
-                    nc.tensor.transpose(t[:, P * i : P * (i + 1)], b2_cols[:, j : j + 1].to_broadcast([P, P]), ident_b[:])
+                    col = b1_cols[:, 8 * c + i : 8 * c + i + 1]
+                    nc.tensor.transpose(t[:, P * i : P * (i + 1)], col.to_broadcast([P, P]), ident_b[:])
+            else:
+                for n in range(2):
+                    add_row(t[:, sl[n]], 1 + c, sl[n])
 
-        def chunk_copy(c):
+        def keep_bias(c):
             nc.scalar.copy(out=b12[:, D * c : D * (c + 1)], in_=pt["bias", c][:])
 
-        def mm2(j, k0, k1):
+        def mm(j, k0, k1):
             b, w, c = j // 8, (j // 4) % 2, j % 4
-            ws = (w1s, w2s)[w]
-            for n in range(2):
-                pt["blk", j, n] = bank((k0, k1)[n], [P, HALF], F32, "blk%d_%d" % (j, n))
+            scales = w2s["t"] if w else w1s
+            for n, k in enumerate((k0, k1)):
+                pt["blk", j, n] = bank(k, [P, HALF], F32, "blk%d_%d" % (j, n))
             for g in range(G):
                 for n in range(2):
-                    w0 = 2048 * c + 1024 * n
+                    col = D * c + HALF * n
                     nc.tensor.matmul_mx(
                         out=pt["blk", j, n][:],
                         lhsT=codes2[b][:, g, :].bitcast(FP8X4), lhsT_scale=scal2[b][:, g, :],
-                        rhs=wc[w][:, g, w0 : w0 + 1024].bitcast(FP4X4),
-                        rhs_scale=ws[:, g, D * c + HALF * n : D * c + HALF * (n + 1)],
+                        rhs=wc[w][:, g, 2 * col : 2 * (col + HALF)].bitcast(FP4X4),
+                        rhs_scale=scales[:, g, col : col + HALF],
                         start=(g == 0), stop=(g == G - 1))
 
-        def bias_of(j, n):
-            c0 = D * (j % 8) + HALF * n
-            return b12[:, c0 : c0 + HALF]
-
         def o_of(j, n):
-            c0 = D * (j % 2) + HALF * n
-            return o[j // 2][:, c0 : c0 + HALF]
+            col = D * (j % 2) + HALF * n
+            return o[j // 2][:, col : col + HALF]
 
-        def ev(j, n):
+        def bias_of(j, n):
+            col = D * (j % 8) + HALF * n
+            return b12[:, col : col + HALF]
+
+        def finish(j, n):
             nc.vector.tensor_tensor(out=o_of(j, n), in0=pt["blk", j, n][:], in1=bias_of(j, n), op=ADD)
 
-        def es(j, n):
+        def fetch(j, n):
             nc.scalar.copy(out=o_of(j, n), in_=pt["blk", j, n][:])
 
-        def eg(j, n):
+        def add_bias(j, n):
             nc.gpsimd.tensor_tensor(out=o_of(j, n), in0=o_of(j, n), in1=bias_of(j, n), op=ADD)
 
-        def put(j, n, width):
+        def store(j, n=0, width=D):
             b, w, c = j // 8, (j // 4) % 2, j % 4
-            d0 = D * c + HALF * n
-            c0 = D * (j % 2) + HALF * n
-            nc.sync.dma_start(out=outs[w][b, :, d0 : d0 + width], in_=o[j // 2][:, c0 : c0 + width])
-
-        def store(j):
-            put(j, 0, D)
-
-        def store_half(j, n):
-            put(j, n, HALF)
-
-        def store_two(j):
-            put(j, 0, 2 * D)
+            dst = outs[w][b, :, D * c + HALF * n : D * c + HALF * n + width]
+            col = D * (j % 2) + HALF * n
+            nc.sync.dma_start(out=dst, in_=o[j // 2][:, col : col + width])
 
         def store_r(b):
             nc.sync.dma_start(out=out_r[b], in_=r[b][:])
 
-        cast_s(0, 1)
-        warm_mm(7)
-        cast_v(0, 0)
+        spin(4)
+        cast(nc.vector.tensor_copy, 0, 0)
+        cast(nc.vector.tensor_copy, 0, 1)
+        zero_w1s()
+        load_scales(w1s, w1_scales)
+        load_words(wc[0], w1_words)
+        load_words(wc[1], w2_words)
+        cast(nc.scalar.copy, 1, 0)
+        cast(nc.scalar.copy, 1, 1)
         turn("hT", hbf, 0, 0, 1)
-        cast_s(1, 1)
-        turn("hT", hbf, 0, 1, 6)
-        cast_v(1, 0)
-        resid_mm(0, 1, 2)
+        turn("hT", hbf, 0, 1, 7)
+        x_plus_bo(0, 0, 0)
+        x_plus_bo(0, 1, 2)
         scale_rows(0, 0)
-        turn("hT", hbf, 1, 1, 4)
         scale_rows(0, 1)
-        turn("hT", hbf, 1, 0, 5)
-        q1(0, 0)
-        resid_copy(0, 1)
-        resid_mm(0, 0, 3)
-        bo_mm(0, 7)
-        q1(0, 1)
-        mm1(0, 0, 6)
-        scale_rows(1, 1)
+        q_h(0, 0)
+        q_h(0, 1)
+        turn("hT", hbf, 1, 0, 4)
+        keep_xb(0, 0)
+        b1_turn(1)
+        turn("hT", hbf, 1, 1, 6)
+        nc.scalar.copy(out=b1_cols[:], in_=pt["b1"][:, 0:32])
+        keep_xb(0, 1)
+        mm_wo(0, 0, 7)
+        mm_wo(0, 1, 3)
         scale_rows(1, 0)
-        resid_copy(0, 0)
-        mm1(0, 1, 4)
-        q1(1, 1)
+        x_plus_bo(1, 0, 2)
+        keep_xb(1, 0)
+        spread("ln2_g", 1, 1)
+
         do_y(0, 0)
-        bo_copy(0)
-        bo_mm(1, 0)
-        bo_copy(1)
-        xb_g(1, 1)
-        chunk_mm(2, 3)
         do_y(0, 1)
-        vec_mm("lng", 1, 2)
-        chunk_mm(1, 7)
-        chunk_copy(2)
-        q1(1, 0)
-        nm_y(0)
-        mm1(1, 1, 0)
-        vec_mm("lnb", 2, 4)
-        chunk_mm(0, 3)
-        sq_y(0)
+        spread("ln2_b", 2, 7)
+        q_h(1, 0)
+        negmean(nmy[0], ysum[0])
+        squares(ssy, y, nmy, 0)
+        scale_rows(1, 1)
+        bias(0, 0)
+        bias(1, 6)
         do_u(0, 0)
-        xb_g(1, 0)
-        chunk_mm(3, 5)
-        rs_y(0)
+        q_h(1, 1)
         do_u(0, 1)
-        chunk_copy(1)
-        do_y(1, 1)
-        mm1(1, 0, 7)
-        vec_mm("fg", 3, 1)
-        chunk_copy(0)
-        do_r(0, 1)
-        chunk_copy(3)
+        zero_w2s()
+        mm_wo(1, 0, 2)
+        rstd(rsy[0], ssy[0])
+        keep_bias(0)
+        keep_bias(1)
+        x_plus_bo(1, 1, 3)
+        keep_xb(1, 1)
+        spread("fln_g", 3, 4)
         do_r(0, 0)
-        nm_r(0)
-        sq_r(0)
+        do_r(0, 1)
+        bias(2, 5)
+        negmean(nmr[0], rsum[0])
+        squares(ssr, r, nmr, 0)
         do_y(1, 0)
-        b2_turn(3)
-        b2_copy()
-        vec_mm("fb", 4, 7)
-        do_v(0, 1)
-        chunk_mm(5, 3)
-        nm_y(1)
-        rs_r(0)
-        sq_y(1)
-        chunk_copy(5)
-        do_v(0, 0)
-        do_u(1, 1)
-        rs_y(1)
-        do_h(0, 0)
-        chunk_mm(6, 0)
-        do_h(0, 1)
-        turn("h2T", h2, 0, 0, 5)
-        turn("h2T", h2, 0, 1, 6)
-        do_u(1, 0)
-        evac_h(0, 0)
-        do_r(1, 1)
-        evac_h(0, 1)
-        chunk_mm(4, 3)
-        q2(0, 0)
-        q2(0, 1)
-        chunk_copy(6)
-        mm2(0, 5, 6)
-        do_r(1, 0)
-        nm_r(1)
-        ev(0, 0)
-        chunk_copy(4)
+        mm_wo(1, 1, 6)
+        load_scales(w2s["t"], w2_scales)
         store_r(0)
-        sq_r(1)
-        do_v(1, 1)
-        mm2(1, 4, 3)
-        mm2(3, 5, 0)
-        es(1, 0)
-        do_v(1, 0)
+        spread("fln_b", 4, 3)
+        bias(3, 0)
+        rstd(rsr[0], ssr[0])
+        keep_bias(2)
+        keep_bias(3)
+        do_v(0, 0)
+        do_v(0, 1)
+        do_y(1, 1)
+        do_h2(0, 0)
+        negmean(nmy[1], ysum[1])
+        squares(ssy, y, nmy, 1)
+        do_h2(0, 1)
+        bias(6, 6)
+        turn("h2T", h2, 0, 0, 2)
+        turn("h2T", h2, 0, 1, 5)
+        bias(4, 0)
+        do_u(1, 0)
+        lay_h2(nc.vector.tensor_copy, 0, 0)
+        lay_h2(nc.scalar.copy, 0, 1)
+        bias(5, 2)
+        rstd(rsy[1], ssy[1])
+        q_h2(0, 0)
+        do_u(1, 1)
+        q_h2(0, 1)
+        keep_bias(4)
+        keep_bias(5)
+        keep_bias(6)
+
+        mm(0, 5, 1)
+        do_r(1, 0)
+        do_r(1, 1)
+        bias(7, 0)
+        fetch(0, 1)
+        negmean(nmr[1], rsum[1])
         store_r(1)
-        rs_r(1)
-        ev(0, 1)
-        ev(1, 1)
-        mm2(6, 2, 4)
-        do_h(1, 1)
-        do_h(1, 0)
-        es(3, 1)
-        mm2(2, 1, 3)
-        es(3, 0)
-        turn("h2T", h2, 1, 0, 7)
-        turn("h2T", h2, 1, 1, 5)
-        ev(6, 0)
-        ev(6, 1)
-        evac_h(1, 1)
-        store_half(0, 0)
-        ev(2, 1)
-        mm2(4, 6, 2)
-        ev(2, 0)
-        q2(1, 1)
-        evac_h(1, 0)
-        q2(1, 0)
-        ev(4, 0)
-        mm2(5, 3, 5)
-        es(4, 1)
-        ev(5, 0)
-        eg(1, 0)
-        mm2(9, 1, 4)
-        ev(5, 1)
-        ev(9, 0)
-        store_half(0, 1)
-        ev(9, 1)
-        mm2(8, 6, 0)
-        ev(8, 0)
-        mm2(10, 5, 1)
-        mm2(11, 7, 4)
+        squares(ssr, r, nmr, 1)
+        mm(1, 7, 2)
+        finish(0, 0)
+        add_bias(0, 1)
+        store(0)
+        do_v(1, 0)
+        rstd(rsr[1], ssr[1])
+        mm(2, 6, 5)
+        finish(1, 0)
+        finish(1, 1)
         store(1)
-        ev(8, 1)
-        ev(10, 1)
-        chunk_mm(7, 6)
-        mm2(7, 0, 3)
-        eg(3, 1)
-        eg(3, 0)
-        store(6)
-        ev(10, 0)
-        mm2(15, 5, 2)
-        chunk_copy(7)
-        ev(11, 0)
-        es(15, 0)
-        ev(11, 1)
-        ev(7, 0)
-        mm2(14, 0, 4)
-        eg(4, 1)
-        ev(7, 1)
-        ev(15, 1)
-        store_two(2)
-        mm2(12, 1, 2)
-        ev(14, 0)
-        store_two(4)
-        eg(15, 0)
-        ev(14, 1)
-        store_two(8)
-        mm2(13, 6, 3)
-        ev(12, 1)
-        store_two(10)
-        es(12, 0)
-        ev(13, 0)
-        ev(13, 1)
-        eg(12, 0)
+        mm(3, 1, 7)
+        finish(2, 0)
+        fetch(2, 1)
+        add_bias(2, 1)
+        keep_bias(7)
+        do_v(1, 1)
+        mm(4, 2, 5)
+        do_h2(1, 0)
+        do_h2(1, 1)
+        store(2)
+        turn("h2T", h2, 1, 0, 6)
+        mm(5, 4, 3)
+        fetch(4, 1)
+        add_bias(4, 1)
+        finish(3, 0)
+        finish(3, 1)
+        store(3)
+        lay_h2(nc.scalar.copy, 1, 0)
+        turn("h2T", h2, 1, 1, 7)
+        finish(4, 0)
+        store(4)
+        mm(6, 6, 5)
+        lay_h2(nc.scalar.copy, 1, 1)
+        finish(5, 0)
+        finish(5, 1)
+        store(5)
+        q_h2(1, 0)
+        q_h2(1, 1)
+        mm(7, 4, 0)
+        fetch(6, 1)
+        add_bias(6, 1)
+        finish(6, 0)
+        finish(7, 0)
+        finish(7, 1)
         store(7)
-        store_two(14)
-        store_two(12)
+        store(6)
+
+        mm(8, 7, 3)
+        finish(8, 0)
+        finish(8, 1)
+        mm(9, 4, 1)
+        finish(9, 0)
+        finish(9, 1)
+        store(8, width=2 * D)
+        mm(10, 5, 6)
+        fetch(10, 0)
+        add_bias(10, 0)
+        finish(10, 1)
+        mm(11, 3, 2)
+        finish(11, 0)
+        finish(11, 1)
+        store(10, width=2 * D)
+        mm(12, 5, 1)
+        finish(12, 0)
+        finish(12, 1)
+        mm(13, 4, 3)
+        finish(13, 0)
+        finish(13, 1)
+        store(12, width=2 * D)
+        mm(14, 5, 0)
+        finish(14, 0)
+        finish(14, 1)
+        store(14)
+        mm(15, 4, 1)
+        finish(15, 0)
+        store(15, n=0, width=HALF)
+        finish(15, 1)
+        store(15, n=1, width=HALF)

from contextlib import ExitStack

import concourse.mybir as mybir
from concourse.masks import make_identity

F32 = mybir.dt.float32
BF16 = mybir.dt.bfloat16
I32 = mybir.dt.int32
U32 = mybir.dt.uint32
U8 = mybir.dt.uint8
FP8 = mybir.dt.float8_e4m3fn
FP8X4 = mybir.dt.float8_e4m3fn_x4
FP4X4 = mybir.dt.float4_e2m1fn_x4
ADD = mybir.AluOpType.add
MULT = mybir.AluOpType.mult
ACT = mybir.ActivationFunctionType

B, T, D, F = 2, 128, 1024, 4096
P = 128
G = D // 512
HALF = 512
EPS = 1e-5

FLOPS = 2 * B * T * D * (D + 2 * F)


def tile_transformerblock_pa_w4_kernel(
    tc, h_bytes, h_scale, x, wo_words, wo_scales, bo, ln2_g, ln2_b, fln_g, fln_b,
    w1_words, w1_scales, b1, w2_words, w2_scales, b2, out_r, out_1, out_2,
):
    nc = tc.nc
    with ExitStack() as ctx:
        sb = ctx.enter_context(tc.tile_pool(name="sb", bufs=1))
        ps = ctx.enter_context(tc.psum_pool(name="ps", bufs=1))
        ctx.enter_context(tc.manual_schedule())

        def bank(i, shape, dtype, name):
            return ps.tile(shape, dtype, tag="bank%d" % i, name=name)

        def pair(shape, dtype, name):
            return [sb.tile(shape, dtype, name="%s%d" % (name, b), align_bytes=64) for b in range(B)]

        vrows = sb.tile([P, D], BF16, name="vrows")
        b1_rows = sb.tile([P, P], BF16, name="b1_rows")
        b1_cols = sb.tile([P, 32], BF16, name="b1_cols")
        ident_f = sb.tile([P, P], F32, name="ident_f")
        ident_b = sb.tile([P, P], BF16, name="ident_b")
        zero = sb.tile([P, HALF], BF16, name="zero")
        one = sb.tile([P, 1], F32, name="one")
        one_out = sb.tile([P, 1], F32, name="one_out")
        wos = sb.tile([P, G, D], U8, name="wos", align_bytes=64)
        w1s = sb.tile([P, G, F], U8, name="w1s", align_bytes=64)

        nc.gpsimd.memset(vrows[:].bitcast(I32), 0)
        make_identity(nc, ident_f[:])
        nc.vector.memset(zero[:].bitcast(I32), 0)
        nc.vector.memset(one[:], 1.0)
        nc.vector.memset(wos[:].bitcast(I32), 0)
        nc.vector.memset(b1_rows[:].bitcast(I32), 0)
        nc.vector.tensor_copy(out=ident_b[:], in_=ident_f[:])
        nc.vector.memset(w1s[:, 0, :].bitcast(I32), 0)

        hb = pair([P, D], U8, "hb")
        xt = pair([P, D], BF16, "xt")
        hs = sb.tile([P, G, 4], F32, name="hs")
        wo = sb.tile([P, G, 2 * D], U8, name="wo", align_bytes=64)
        wc = pair([P, G, 2 * F], U8, "wc")
        b12 = sb.tile([P, 2 * F], BF16, name="b12")

        def load_words(dst, src):
            nc.sync.dma_start(out=dst[:].bitcast(I32), in_=src.bitcast(I32).rearrange("g p n -> p g n"))

        def load_scales(dst, src):
            words = src.bitcast(I32).rearrange("g (q r) n -> r q g n", r=4)
            for r in range(4):
                nc.sync.dma_start(out=dst[r:P:32, :, :].bitcast(I32), in_=words[r])

        def load_row(dst, vec):
            nc.scalar.dma_start(out=dst, in_=vec.rearrange("(o c) -> o c", o=1))

        nc.sync.dma_start(out=hb[0][:], in_=h_bytes[0])
        nc.scalar.dma_start(out=hs[:], in_=h_scale.rearrange("a o (g p t) -> p (a o g) t", p=P, t=4))
        load_row(vrows[0:1, :], bo)
        nc.sync.dma_start(out=hb[1][:], in_=h_bytes[1])
        nc.sync.dma_start(out=xt[0][:], in_=x[0])
        load_words(wo, wo_words)
        for i, vec in enumerate((ln2_g, ln2_b, fln_g, fln_b), start=1):
            load_row(vrows[i : i + 1, :], vec)
        nc.scalar.dma_start(out=vrows[5:9, :], in_=b2.rearrange("(r c) -> r c", r=4))
        nc.scalar.dma_start(out=b1_rows[0:32, :], in_=b1.rearrange("(r c) -> r c", r=32))
        nc.scalar.activation(out=one_out[:], in_=one[:], func=ACT.Abs_reciprocal_sqrt, bias=EPS, scale=1.0)
        load_scales(wos, wo_scales)
        nc.sync.dma_start(out=xt[1][:], in_=x[1])

        hbf = pair([P, D], BF16, "hbf")
        qin = [
            sb.tile([P, G, P, 4], BF16, name="qin%d" % b, tag=("qin0", "qin1_then_w2s")[b], align_bytes=64)
            for b in range(B)
        ]
        codes = pair([P, G, P], U32, "codes")
        scal = pair([P, G, P], U8, "scal")
        qin2 = pair([P, G, P, 4], BF16, "qin2_")
        codes2 = pair([P, G, P], U32, "codes2_")
        scal2 = pair([P, G, P], U8, "scal2_")
        xb = pair([P, D], F32, "xb")
        y = pair([P, D], F32, "y")
        u = pair([P, D], F32, "u")
        r = pair([P, D], F32, "r")
        v = pair([P, D], F32, "v")
        h2 = pair([P, D], BF16, "h2_")
        sq = pair([P, D], BF16, "sq")
        o = [sb.tile([P, 2 * D], F32, name="o%d" % m) for m in range(8)]

        ysum, rsum = pair([P, 2], F32, "ysum"), pair([P, 2], F32, "rsum")
        nmy, nmr = pair([P, 1], F32, "nmy"), pair([P, 1], F32, "nmr")
        ssy, ssr = pair([P, 1], F32, "ssy"), pair([P, 1], F32, "ssr")
        rsy, rsr = pair([P, 1], F32, "rsy"), pair([P, 1], F32, "rsr")

        sl = [slice(0, HALF), slice(HALF, D)]
        outs = (out_1, out_2)
        pt = {}
        w2s = {}

        def spin(k):
            pt["spin"] = bank(k, [P, HALF], F32, "spin")
            for _ in range(4):
                nc.tensor.matmul(pt["spin"][:], lhsT=zero[:, 0:P], rhs=zero[:], start=True, stop=True)

        def zero_w1s():
            nc.vector.memset(w1s[:, 1, :].bitcast(I32), 0)

        def zero_w2s():
            w2s["t"] = sb.tile([P, G, F], U8, name="w2s", tag="qin1_then_w2s", align_bytes=64)
            nc.gpsimd.memset(w2s["t"][:].bitcast(I32), 0)

        def cast(copy, b, n):
            copy(out=hbf[b][:, sl[n]], in_=hb[b][:, sl[n]].bitcast(FP8))

        def turn(kind, src, b, g, k):
            t = bank(k, [P, 2, P], F32, "%s%d_%d" % (kind, b, g))
            pt[kind, b, g] = t
            words = src[b][:].bitcast(F32)
            for e in range(2):
                nc.tensor.transpose(t[:, e, :], words[:, 256 * g + e : 256 * (g + 1) : 2], ident_f[:])

        def add_row(dst, row, cols, start=True):
            nc.tensor.matmul(
                dst, lhsT=ident_b[:, row : row + 1].to_broadcast([P, P]), rhs=vrows[:, cols], start=start, stop=True)

        def x_plus_bo(b, n, k):
            t = bank(k, [P, HALF], F32, "xb_ps%d_%d" % (b, n))
            pt["xb", b, n] = t
            nc.tensor.matmul(t[:], lhsT=ident_b[:], rhs=xt[b][:, sl[n]], start=True, stop=False)
            add_row(t[:], 0, sl[n], start=False)

        def keep_xb(b, n):
            nc.scalar.copy(out=xb[b][:, sl[n]], in_=pt["xb", b, n][:])

        def scale_rows(b, g):
            src = pt["hT", b, g][:].bitcast(BF16).rearrange("p k (n e) -> p n k e", e=2)
            fac = hs[:, g, :].rearrange("p (k e) -> p k e", e=2).unsqueeze(1).to_broadcast([P, P, 2, 2])
            nc.vector.tensor_tensor(
                out=qin[b][:, g, :, :].rearrange("p n (k e) -> p n k e", e=2), in0=src, in1=fac, op=MULT)

        def quantise(dst, scales, src, g):
            nc.vector.quantize_mx(
                out=dst[:, g, :].bitcast(FP8X4), scales=scales[:, g, :],
                in_=src[:, g, :, :].rearrange("p n t -> p (n t)"))

        def q_h(b, g):
            quantise(codes[b], scal[b], qin[b], g)

        def q_h2(b, g):
            quantise(codes2[b], scal2[b], qin2[b], g)

        def mm_wo(b, n, k):
            pt["acc", b, n] = bank(k, [P, HALF], F32, "acc%d_%d" % (b, n))
            for g in range(G):
                nc.tensor.matmul_mx(
                    out=pt["acc", b, n][:],
                    lhsT=codes[b][:, g, :].bitcast(FP8X4), lhsT_scale=scal[b][:, g, :],
                    rhs=wo[:, g, 2 * HALF * n : 2 * HALF * (n + 1)].bitcast(FP4X4), rhs_scale=wos[:, g, sl[n]],
                    start=(g == 0), stop=(g == G - 1))

        def spread(name, row, k):
            pt[name] = bank(k, [P, D], BF16, name)
            for n in range(2):
                add_row(pt[name][:, sl[n]], row, sl[n])

        def do_y(b, n):
            nc.vector.scalar_tensor_tensor(
                out=y[b][:, sl[n]], in0=pt["acc", b, n][:], scalar=1.0, in1=xb[b][:, sl[n]], op0=MULT, op1=ADD,
                accum_out=ysum[b][:, n : n + 1])

        def negmean(dst, sums):
            nc.vector.tensor_scalar(
                out=dst[:], in0=sums[:, 0:1], scalar1=sums[:, 1:2], scalar2=-1.0 / D, op0=ADD, op1=MULT)

        def squares(total, src, nm, b):
            nc.scalar.activation(
                out=sq[b][:], in_=src[b][:], func=ACT.Square, bias=nm[b][:], scale=1.0, accum_out=total[b][:])

        def rstd(dst, total):
            nc.scalar.activation(out=dst[:], in_=total[:], func=ACT.Abs_reciprocal_sqrt, bias=EPS, scale=1.0 / D)

        def centre(dst, src, nm, gain, b, n):
            nc.vector.scalar_tensor_tensor(
                out=dst[b][:, sl[n]], in0=src[b][:, sl[n]], scalar=nm[b][:], in1=pt[gain][:, sl[n]], op0=ADD, op1=MULT)

        def do_u(b, n):
            centre(u, y, nmy, "ln2_g", b, n)

        def do_v(b, n):
            centre(v, r, nmr, "fln_g", b, n)

        def do_r(b, n):
            nc.vector.scalar_tensor_tensor(
                out=r[b][:, sl[n]], in0=u[b][:, sl[n]], scalar=rsy[b][:], in1=pt["ln2_b"][:, sl[n]], op0=MULT, op1=ADD,
                accum_out=rsum[b][:, n : n + 1])

        def do_h2(b, n):
            nc.vector.scalar_tensor_tensor(
                out=h2[b][:, sl[n]], in0=v[b][:, sl[n]], scalar=rsr[b][:], in1=pt["fln_b"][:, sl[n]], op0=MULT, op1=ADD)

        def lay_h2(copy, b, g):
            copy(
                out=qin2[b][:, g, :, :].rearrange("p n t -> p (n t)").bitcast(F32).rearrange("p (n k) -> p n k", k=2),
                in_=pt["h2T", b, g][:].rearrange("p k n -> p n k"))

        def b1_turn(k):
            pt["b1"] = bank(k, [P, P], BF16, "b1_t")
            nc.tensor.transpose(pt["b1"][:], b1_rows[:], ident_b[:])

        def bias(c, k):
            t = bank(k, [P, D], BF16, "bias%d" % c)
            pt["bias", c] = t
            if c < 4:
                for i in range(8):
                    col = b1_cols[:, 8 * c + i : 8 * c + i + 1]
                    nc.tensor.transpose(t[:, P * i : P * (i + 1)], col.to_broadcast([P, P]), ident_b[:])
            else:
                for n in range(2):
                    add_row(t[:, sl[n]], 1 + c, sl[n])

        def keep_bias(c):
            nc.scalar.copy(out=b12[:, D * c : D * (c + 1)], in_=pt["bias", c][:])

        def mm(j, k0, k1):
            b, w, c = j // 8, (j // 4) % 2, j % 4
            scales = w2s["t"] if w else w1s
            for n, k in enumerate((k0, k1)):
                pt["blk", j, n] = bank(k, [P, HALF], F32, "blk%d_%d" % (j, n))
            for g in range(G):
                for n in range(2):
                    col = D * c + HALF * n
                    nc.tensor.matmul_mx(
                        out=pt["blk", j, n][:],
                        lhsT=codes2[b][:, g, :].bitcast(FP8X4), lhsT_scale=scal2[b][:, g, :],
                        rhs=wc[w][:, g, 2 * col : 2 * (col + HALF)].bitcast(FP4X4),
                        rhs_scale=scales[:, g, col : col + HALF],
                        start=(g == 0), stop=(g == G - 1))

        def o_of(j, n):
            col = D * (j % 2) + HALF * n
            return o[j // 2][:, col : col + HALF]

        def bias_of(j, n):
            col = D * (j % 8) + HALF * n
            return b12[:, col : col + HALF]

        def finish(j, n):
            nc.vector.tensor_tensor(out=o_of(j, n), in0=pt["blk", j, n][:], in1=bias_of(j, n), op=ADD)

        def fetch(j, n):
            nc.scalar.copy(out=o_of(j, n), in_=pt["blk", j, n][:])

        def add_bias(j, n):
            nc.gpsimd.tensor_tensor(out=o_of(j, n), in0=o_of(j, n), in1=bias_of(j, n), op=ADD)

        def store(j, n=0, width=D):
            b, w, c = j // 8, (j // 4) % 2, j % 4
            dst = outs[w][b, :, D * c + HALF * n : D * c + HALF * n + width]
            col = D * (j % 2) + HALF * n
            nc.sync.dma_start(out=dst, in_=o[j // 2][:, col : col + width])

        def store_r(b):
            nc.sync.dma_start(out=out_r[b], in_=r[b][:])

        spin(4)
        cast(nc.vector.tensor_copy, 0, 0)
        cast(nc.vector.tensor_copy, 0, 1)
        zero_w1s()
        load_scales(w1s, w1_scales)
        load_words(wc[0], w1_words)
        load_words(wc[1], w2_words)
        cast(nc.scalar.copy, 1, 0)
        cast(nc.scalar.copy, 1, 1)
        turn("hT", hbf, 0, 0, 1)
        turn("hT", hbf, 0, 1, 7)
        x_plus_bo(0, 0, 0)
        x_plus_bo(0, 1, 2)
        scale_rows(0, 0)
        scale_rows(0, 1)
        q_h(0, 0)
        q_h(0, 1)
        turn("hT", hbf, 1, 0, 4)
        keep_xb(0, 0)
        b1_turn(1)
        turn("hT", hbf, 1, 1, 6)
        nc.scalar.copy(out=b1_cols[:], in_=pt["b1"][:, 0:32])
        keep_xb(0, 1)
        mm_wo(0, 0, 7)
        mm_wo(0, 1, 3)
        scale_rows(1, 0)
        x_plus_bo(1, 0, 2)
        keep_xb(1, 0)
        spread("ln2_g", 1, 1)

        do_y(0, 0)
        do_y(0, 1)
        spread("ln2_b", 2, 7)
        q_h(1, 0)
        negmean(nmy[0], ysum[0])
        squares(ssy, y, nmy, 0)
        scale_rows(1, 1)
        bias(0, 0)
        bias(1, 6)
        do_u(0, 0)
        q_h(1, 1)
        do_u(0, 1)
        zero_w2s()
        mm_wo(1, 0, 2)
        rstd(rsy[0], ssy[0])
        keep_bias(0)
        keep_bias(1)
        x_plus_bo(1, 1, 3)
        keep_xb(1, 1)
        spread("fln_g", 3, 4)
        do_r(0, 0)
        do_r(0, 1)
        bias(2, 5)
        negmean(nmr[0], rsum[0])
        squares(ssr, r, nmr, 0)
        do_y(1, 0)
        mm_wo(1, 1, 6)
        load_scales(w2s["t"], w2_scales)
        store_r(0)
        spread("fln_b", 4, 3)
        bias(3, 0)
        rstd(rsr[0], ssr[0])
        keep_bias(2)
        keep_bias(3)
        do_v(0, 0)
        do_v(0, 1)
        do_y(1, 1)
        do_h2(0, 0)
        negmean(nmy[1], ysum[1])
        squares(ssy, y, nmy, 1)
        do_h2(0, 1)
        bias(6, 6)
        turn("h2T", h2, 0, 0, 2)
        turn("h2T", h2, 0, 1, 5)
        bias(4, 0)
        do_u(1, 0)
        lay_h2(nc.vector.tensor_copy, 0, 0)
        lay_h2(nc.scalar.copy, 0, 1)
        bias(5, 2)
        rstd(rsy[1], ssy[1])
        q_h2(0, 0)
        do_u(1, 1)
        q_h2(0, 1)
        keep_bias(4)
        keep_bias(5)
        keep_bias(6)

        mm(0, 5, 1)
        do_r(1, 0)
        do_r(1, 1)
        bias(7, 0)
        fetch(0, 1)
        negmean(nmr[1], rsum[1])
        store_r(1)
        squares(ssr, r, nmr, 1)
        mm(1, 7, 2)
        finish(0, 0)
        add_bias(0, 1)
        store(0)
        do_v(1, 0)
        rstd(rsr[1], ssr[1])
        mm(2, 6, 5)
        finish(1, 0)
        finish(1, 1)
        store(1)
        mm(3, 1, 7)
        finish(2, 0)
        fetch(2, 1)
        add_bias(2, 1)
        keep_bias(7)
        do_v(1, 1)
        mm(4, 2, 5)
        do_h2(1, 0)
        do_h2(1, 1)
        store(2)
        turn("h2T", h2, 1, 0, 6)
        mm(5, 4, 3)
        fetch(4, 1)
        add_bias(4, 1)
        finish(3, 0)
        finish(3, 1)
        store(3)
        lay_h2(nc.scalar.copy, 1, 0)
        turn("h2T", h2, 1, 1, 7)
        finish(4, 0)
        store(4)
        mm(6, 6, 5)
        lay_h2(nc.scalar.copy, 1, 1)
        finish(5, 0)
        finish(5, 1)
        store(5)
        q_h2(1, 0)
        q_h2(1, 1)
        mm(7, 4, 0)
        fetch(6, 1)
        add_bias(6, 1)
        finish(6, 0)
        finish(7, 0)
        finish(7, 1)
        store(7)
        store(6)

        mm(8, 7, 3)
        finish(8, 0)
        finish(8, 1)
        mm(9, 4, 1)
        finish(9, 0)
        finish(9, 1)
        store(8, width=2 * D)
        mm(10, 5, 6)
        fetch(10, 0)
        add_bias(10, 0)
        finish(10, 1)
        mm(11, 3, 2)
        finish(11, 0)
        finish(11, 1)
        store(10, width=2 * D)
        mm(12, 5, 1)
        finish(12, 0)
        finish(12, 1)
        mm(13, 4, 3)
        finish(13, 0)
        finish(13, 1)
        store(12, width=2 * D)
        mm(14, 5, 0)
        finish(14, 0)
        finish(14, 1)
        store(14)
        mm(15, 4, 1)
        finish(15, 0)
        store(15, n=0, width=HALF)
        finish(15, 1)
        store(15, n=1, width=HALF)
